import numpy as np
import ml_dtypes


def mxq(x, axis, fmt="e4m3"):
    dtype, down = {"e4m3": (ml_dtypes.float8_e4m3fn, 7), "e5m2": (ml_dtypes.float8_e5m2, 14)}[fmt]
    v = np.moveaxis(np.asarray(x, np.float32).astype(ml_dtypes.bfloat16).astype(np.float64), axis, -1)
    blocks = v.reshape(v.shape[:-1] + (-1, 32))
    amax = np.abs(blocks).max(-1, keepdims=True)
    byte = np.maximum(np.where(amax > 0, np.frexp(amax)[1] - 1 + 127, 0) - down, 1)
    scale = np.exp2(byte - 127.0)
    codes = (blocks / scale).astype(np.float32).astype(dtype).astype(np.float64)
    return np.moveaxis((codes * scale).reshape(v.shape), -1, axis)


WIDE = False


def mx_kscale(k):
    if not WIDE:
        return np.ones(k)
    levels = np.array([20, -20, 10, -10, 0])
    a = np.random.permutation(np.resize(levels, k // 512 * 4)).reshape(k // 512, 4)
    idx = np.arange(k)
    return np.exp2(a[idx // 512, idx % 128 // 32])


BF16 = ml_dtypes.bfloat16


def bf(x):
    return np.asarray(x, np.float32).astype(BF16)


def f64(x):
    return np.asarray(x).astype(np.float64)


B, S, DI, DO = 4, 256, 2048, 2048
R = B * S
LN_EPS = 1e-5


def ste_sign(w):
    return np.where(w >= 0, 1.0, -1.0)


def pre_norm(x, weight, in_channel_scale, out_channel_scale, bias):
    xs = f64(x).reshape(R, DI) * f64(in_channel_scale)
    return (xs @ ste_sign(f64(weight)).T) * f64(out_channel_scale) + f64(bias)


def row_stats(h):
    mu = np.mean(h, axis=1, keepdims=True)
    var = np.mean(np.square(h - mu), axis=1, keepdims=True)
    return mu, 1.0 / np.sqrt(var + LN_EPS)


def setup_inputs():
    r = np.asarray(mx_kscale(DO), np.float64)[np.arange(R) * DO // R].reshape(B, S, 1)
    x0 = bf(np.random.standard_normal((B, S, DI)))
    weight = bf(np.random.standard_normal((DO, DI)) * 0.02)
    ics = bf(np.random.uniform(0.5, 1.5, DI) / np.sqrt(DI))
    ocs = bf(np.random.uniform(0.5, 1.5, DO))
    bias = bf(np.random.standard_normal(DO) * 0.3)
    gamma = bf(1.0 + 0.1 * np.random.standard_normal(DO))
    beta = bf(0.1 * np.random.standard_normal(DO))
    g = bf(np.random.standard_normal((B, S, DO)) * np.exp2(np.random.randint(-12, 1, (B, S, 1))) * 0.02 * r)
    h = pre_norm(x0, weight, ics, ocs, bias)
    mu, rstd = row_stats(h)
    return {"x": bf(f64(x0) / r), "weight": weight, "in_channel_scale": ics, "out_channel_scale": ocs,
            "bias": bias, "ln_gamma": gamma, "ln_beta": beta,
            "h": np.asarray(h, np.float32), "mu": np.asarray(mu, np.float32),
            "rstd": np.asarray(rstd, np.float32), "grad_out": g}


def reference(x, weight, in_channel_scale, out_channel_scale, bias, ln_gamma, ln_beta, h, mu, rstd, grad_out):
    xf = f64(x).reshape(R, DI)
    g = f64(grad_out).reshape(R, DO)
    rs = f64(rstd)
    xhat = (f64(h) - f64(mu)) * rs
    gy = g * f64(ln_gamma)
    c1 = np.mean(gy, axis=1, keepdims=True)
    c2 = np.mean(gy * xhat, axis=1, keepdims=True)
    dm = (gy - c1 - xhat * c2) * rs * f64(out_channel_scale)
    w_bin = ste_sign(f64(weight))
    dxs = mxq(dm, 1, "e5m2") @ mxq(w_bin, 0, "e4m3")
    return np.sum(xf * dxs, axis=0)

@@ -1,0 +1,274 @@
+from contextlib import ExitStack
+
+import concourse.mybir as mybir
+from concourse.masks import make_identity
+
+F32 = mybir.dt.float32
+BF16 = mybir.dt.bfloat16
+U32 = mybir.dt.uint32
+U8 = mybir.dt.uint8
+E4M3_X4 = mybir.dt.float8_e4m3fn_x4
+E5M2_X4 = mybir.dt.float8_e5m2_x4
+ALU = mybir.AluOpType
+ACT = mybir.ActivationFunctionType
+
+P = 128
+PACK = 4
+TOKENS = 1024
+D_IN = 2048
+D_OUT = 2048
+TILES = TOKENS // P
+PASSES = D_OUT // (P * PACK)
+BLOCKS = D_OUT // P
+N_TILE = 512
+CHUNKS = D_IN // N_TILE
+W_LOADS = 2 * CHUNKS
+AHEAD = 2
+
+FLOPS = 2 * TOKENS * D_IN * D_OUT
+
+
+def tile_onebitlinear_v_kernel(
+    tc, x, weight, in_channel_scale, out_channel_scale, bias, ln_gamma, ln_beta, h, mu, rstd, grad_out, out
+):
+    nc = tc.nc
+    with ExitStack() as stack:
+        keep = stack.enter_context(tc.tile_pool(name="keep", bufs=1))
+        rows = stack.enter_context(tc.tile_pool(name="rows", bufs=3))
+        small = stack.enter_context(tc.tile_pool(name="small", bufs=4))
+        stage = stack.enter_context(tc.tile_pool(name="stage", bufs=2))
+        turned = stack.enter_context(tc.psum_pool(name="turned", bufs=4))
+        banks = stack.enter_context(tc.psum_pool(name="banks", bufs=3))
+        total = stack.enter_context(tc.psum_pool(name="total", bufs=1))
+        stack.enter_context(tc.manual_schedule())
+
+        g_view = grad_out.flatten_outer_dims().rearrange("(p n) d -> p n d", n=TILES)
+        x_view = x.flatten_outer_dims().rearrange("(p n) d -> p n d", n=TILES)
+        h_view = h.rearrange("(p n) d -> p n d", n=TILES)
+        w_view = weight.rearrange("(r p) i -> p r i", p=P)
+
+        x_all = keep.tile([P, TILES, D_IN], BF16)
+        w_codes = keep.tile([P, CHUNKS, PASSES, N_TILE], U32, align_bytes=64)
+        w_scales = keep.tile([P, CHUNKS, PASSES, N_TILE], U8, align_bytes=64)
+        dm_codes = keep.tile([P, TILES, PASSES, P], U32, align_bytes=64)
+        dm_scales = keep.tile([P, TILES, PASSES, P], U8, align_bytes=64)
+        column_sums = total.tile([P, TILES, CHUNKS * PACK], F32)
+        g_of, h_of, gr_of, sums_of, line_of, banks_of, grouped_of = {}, {}, {}, {}, {}, {}, {}
+        raw_of, signs_of, acc_of, product_of = {}, {}, {}, {}
+
+        def load_rows(n):
+            g_of[n] = rows.tile([P, D_OUT], BF16, tag="g", name="g_tile")
+            nc.sync.dma_start(out=g_of[n][:], in_=g_view[:, n, :])
+            h_of[n] = rows.tile([P, D_OUT], F32, tag="h", name="h_tile", bufs=4)
+            nc.sync.dma_start(out=h_of[n][:], in_=h_view[:, n, :])
+
+        def load_x(n):
+            nc.sync.dma_start(out=x_all[:, n, :], in_=x_view[:, n, :])
+
+        def scaled_gradient(n):
+            sums_of[n] = small.tile([P, 2], F32, tag="sums", name="sums")
+            gr_of[n] = rows.tile([P, D_OUT], F32, tag="gr", name="gr")
+            nc.vector.scalar_tensor_tensor(
+                out=gr_of[n][:], in0=g_of[n][:], scalar=rstd_sb[:, n : n + 1], in1=gamma_all[:],
+                op0=ALU.mult, op1=ALU.mult, accum_out=sums_of[n][:, 0:1],
+            )
+
+        def row_sums(n):
+            unread = stage.tile([P, D_OUT], F32, tag="unread", bufs=1)
+            nc.vector.scalar_tensor_tensor(
+                out=unread[:], in0=h_of[n][:], scalar=mu_sb[:, n : n + 1], in1=gr_of[n][:],
+                op0=ALU.subtract, op1=ALU.mult, accum_out=sums_of[n][:, 1:2],
+            )
+            line_of[n] = small.tile([P, 3], F32, tag="line", name="line")
+            nc.vector.tensor_scalar(
+                out=line_of[n][:, 0:2], in0=slope_of[:, n, :], scalar1=sums_of[n][:, 1:2], scalar2=None, op0=ALU.mult
+            )
+            nc.vector.scalar_tensor_tensor(
+                out=line_of[n][:, 2:3], in0=sums_of[n][:, 0:1], scalar=-1.0 / D_OUT, in1=line_of[n][:, 1:2],
+                op0=ALU.mult, op1=ALU.add,
+            )
+
+        def straight_line(n):
+            nc.scalar.activation(
+                out=h_of[n][:], in_=h_of[n][:], func=ACT.Identity, bias=line_of[n][:, 2:3], scale=line_of[n][:, 0:1]
+            )
+
+        def turn(n):
+            banks_of[n] = []
+            for c in range(PASSES):
+                bank = turned.tile([P, PACK, P], F32, tag="turned")
+                banks_of[n].append(bank)
+                for j in range(PACK):
+                    cols = slice((c * PACK + j) * P, (c * PACK + j + 1) * P)
+                    nc.tensor.matmul(
+                        out=bank[:, j, :], lhsT=gr_of[n][:, cols], rhs=identity[:], is_transpose=True,
+                        start=True, stop=False,
+                    )
+                    nc.tensor.matmul(
+                        out=bank[:, j, :], lhsT=h_of[n][:, cols], rhs=identity[:], is_transpose=True,
+                        start=False, stop=True,
+                    )
+
+        def scale_round(n):
+            grouped_of[n] = stage.tile([P, PASSES, P, PACK], BF16, tag="grouped", name="grouped", align_bytes=64)
+            for c in range(PASSES):
+                nc.vector.tensor_tensor(
+                    out=grouped_of[n][:, c, :, :],
+                    in0=banks_of[n][c][:].rearrange("p j t -> p t j"),
+                    in1=ocs_col[:, c * PACK : (c + 1) * PACK].unsqueeze(1).to_broadcast([P, P, PACK]),
+                    op=ALU.mult,
+                )
+
+        def quantise_rows(n):
+            nc.vector.quantize_mx(
+                out=dm_codes[:, n, :, :].rearrange("p c t -> p (c t)").bitcast(E5M2_X4),
+                scales=dm_scales[:, n, :, :].rearrange("p c t -> p (c t)"),
+                in_=grouped_of[n][:].rearrange("p c t j -> p (c t j)"),
+            )
+
+        def load_weights(load):
+            chunk, half = divmod(load, 2)
+            raw_of[load] = stage.tile([P, 2 * PACK, N_TILE], BF16, tag="raw", name="raw")
+            nc.scalar.dma_start(
+                out=raw_of[load][:],
+                in_=w_view[:, half * 2 * PACK : (half + 1) * 2 * PACK, chunk * N_TILE : (chunk + 1) * N_TILE],
+            )
+
+        def weight_signs(chunk, c):
+            signs_of[chunk, c] = stage.tile([P, N_TILE, PACK], BF16, tag="signs", name="signs", bufs=4, align_bytes=64)
+            k = c % 2
+            nc.scalar.activation(
+                out=signs_of[chunk, c][:].rearrange("p (u i) j -> p u j i", i=4),
+                in_=raw_of[2 * chunk + c // 2][:, k * PACK : (k + 1) * PACK, :].rearrange("p j (u i) -> p u j i", i=4),
+                func=ACT.Sign, scale=2.0**120, bias=2.0**-20,
+            )
+
+        def weight_pair(load):
+            chunk, half = divmod(load, 2)
+            weight_signs(chunk, 2 * half)
+            weight_signs(chunk, 2 * half + 1)
+            if load + 2 < W_LOADS:
+                load_weights(load + 2)
+
+        def quantise_weights(chunk, c):
+            nc.vector.quantize_mx(
+                out=w_codes[:, chunk, c, :].bitcast(E4M3_X4),
+                scales=w_scales[:, chunk, c, :],
+                in_=signs_of[chunk, c][:].rearrange("p w j -> p (w j)"),
+            )
+
+        def multiply(n, chunk):
+            acc_of[n, chunk] = banks.tile([P, N_TILE], F32, tag="acc", name="acc")
+            for c in range(PASSES):
+                nc.tensor.matmul_mx(
+                    out=acc_of[n, chunk][:],
+                    lhsT=dm_codes[:, n, c, :].bitcast(E5M2_X4),
+                    lhsT_scale=dm_scales[:, n, c, :],
+                    rhs=w_codes[:, chunk, c, :].bitcast(E4M3_X4),
+                    rhs_scale=w_scales[:, chunk, c, :],
+                    start=(c == 0),
+                    stop=(c == PASSES - 1),
+                )
+
+        def times_x(n, chunk):
+            product_of[n, chunk] = stage.tile([P, N_TILE], F32, tag="product", name="product", bufs=7)
+            nc.vector.tensor_tensor(
+                out=product_of[n, chunk][:], in0=acc_of[n, chunk][:],
+                in1=x_all[:, n, chunk * N_TILE : (chunk + 1) * N_TILE], op=ALU.mult,
+            )
+
+        def add_tokens(n, chunk):
+            for b in range(PACK):
+                col = chunk * PACK + b
+                nc.tensor.matmul(
+                    out=column_sums[:, n, col : col + 1], lhsT=product_of[n, chunk][:, b * P : (b + 1) * P],
+                    rhs=ones[:], start=True, stop=True,
+                )
+
+        def cells_ready_after(s):
+            return [(n, chunk) for n in range(TILES) for chunk in range(CHUNKS) if max(n, chunk) == s]
+
+        rstd_sb = keep.tile([P, TILES], F32)
+        nc.sync.dma_start(out=rstd_sb[:], in_=rstd.rearrange("(p n) o -> p (n o)", n=TILES))
+        mu_sb = keep.tile([P, TILES], F32)
+        nc.sync.dma_start(out=mu_sb[:], in_=mu.rearrange("(p n) o -> p (n o)", n=TILES))
+        gamma_all = keep.tile([P, D_OUT], BF16)
+        nc.scalar.dma_start(out=gamma_all[:], in_=ln_gamma.partition_broadcast(P))
+        ocs_rows = keep.tile([BLOCKS, P], BF16)
+        nc.sync.dma_start(out=ocs_rows[:], in_=out_channel_scale.rearrange("(b p) -> b p", p=P))
+        load_rows(0)
+        load_weights(0)
+        load_rows(1)
+        load_weights(1)
+        load_rows(2)
+
+        identity = keep.tile([P, P], F32)
+        make_identity(nc, identity[:])
+        ones = keep.tile([P, 1], F32)
+        nc.vector.memset(ones[:], 1.0)
+        ocs_square = keep.tile([P, P], F32)
+        nc.vector.memset(ocs_square[:], 0.0)
+        out_square = keep.tile([P, P], F32)
+        nc.vector.memset(out_square[:], 0.0)
+
+        slope_of = keep.tile([P, TILES, 2], F32)
+        nc.vector.scalar_tensor_tensor(
+            out=slope_of[:, :, 0], in0=rstd_sb[:], scalar=-1.0 / D_OUT, in1=rstd_sb[:], op0=ALU.mult, op1=ALU.mult
+        )
+        nc.vector.scalar_tensor_tensor(
+            out=slope_of[:, :, 1], in0=slope_of[:, :, 0], scalar=-1.0, in1=mu_sb[:], op0=ALU.mult, op1=ALU.mult
+        )
+
+        nc.vector.tensor_copy(out=ocs_square[0:BLOCKS, :], in_=ocs_rows[:])
+        ocs_turned = turned.tile([P, PACK, P], F32, tag="turned")
+        nc.tensor.transpose(ocs_turned[:, 0, :], ocs_square[:], identity[:])
+        ocs_col = keep.tile([P, BLOCKS], F32)
+        nc.vector.tensor_copy(out=ocs_col[:], in_=ocs_turned[:, 0, 0:BLOCKS])
+
+        weight_pair(0)
+        for n in range(AHEAD):
+            scaled_gradient(n)
+            row_sums(n)
+            straight_line(n)
+
+        turn(0)
+
+        for s in range(TILES):
+            later = s + AHEAD
+            if later + 1 < TILES:
+                load_rows(later + 1)
+            load_x(s)
+            if 2 * s + 1 < W_LOADS:
+                weight_pair(2 * s + 1)
+            if later < TILES:
+                scaled_gradient(later)
+                row_sums(later)
+                straight_line(later)
+            if 2 * s + 2 < W_LOADS:
+                weight_pair(2 * s + 2)
+            scale_round(s)
+            if s < CHUNKS:
+                for c in range(PASSES):
+                    quantise_weights(s, c)
+            quantise_rows(s)
+            for n, chunk in cells_ready_after(s - 1):
+                times_x(n, chunk)
+            if s + 1 < TILES:
+                turn(s + 1)
+            for n, chunk in cells_ready_after(s - 1):
+                add_tokens(n, chunk)
+            for n, chunk in cells_ready_after(s):
+                multiply(n, chunk)
+        for n, chunk in cells_ready_after(TILES - 1):
+            times_x(n, chunk)
+            add_tokens(n, chunk)
+
+        nc.vector.tensor_reduce(
+            out=out_square[:, 0 : CHUNKS * PACK], in_=column_sums[:].rearrange("p n c -> p c n"),
+            axis=mybir.AxisListType.X, op=ALU.add,
+        )
+        out_turned = turned.tile([P, PACK, P], F32, tag="turned")
+        nc.tensor.transpose(out_turned[:, 0, :], out_square[:], identity[:])
+        result = keep.tile([P, P], F32)
+        nc.vector.tensor_copy(out=result[:], in_=out_turned[:, 0, :])
+        nc.sync.dma_start(out=out.rearrange("(c p) -> c p", p=P), in_=result[0 : CHUNKS * PACK, :])

@@ -24,6 +24,7 @@ N_TILE = 512
 CHUNKS = D_IN // N_TILE
 W_LOADS = 2 * CHUNKS
 AHEAD = 2
+TURN_LEAD = 2
 
 FLOPS = 2 * TOKENS * D_IN * D_OUT
 
@@ -52,12 +53,13 @@ def tile_onebitlinear_v_kernel(
         w_scales = keep.tile([P, CHUNKS, PASSES, N_TILE], U8, align_bytes=64)
         dm_codes = keep.tile([P, TILES, PASSES, P], U32, align_bytes=64)
         dm_scales = keep.tile([P, TILES, PASSES, P], U8, align_bytes=64)
-        column_sums = total.tile([P, TILES, CHUNKS * PACK], F32)
+        column_sums = total.tile([P, CHUNKS * PACK], F32)
+        running = keep.tile([P, D_IN], F32)
         g_of, h_of, gr_of, sums_of, line_of, banks_of, grouped_of = {}, {}, {}, {}, {}, {}, {}
-        raw_of, signs_of, acc_of, product_of = {}, {}, {}, {}
+        raw_of, signs_of, acc_of = {}, {}, {}
 
         def load_rows(n):
-            g_of[n] = rows.tile([P, D_OUT], BF16, tag="g", name="g_tile")
+            g_of[n] = rows.tile([P, D_OUT], BF16, tag="g", name="g_tile", bufs=2)
             nc.sync.dma_start(out=g_of[n][:], in_=g_view[:, n, :])
             h_of[n] = rows.tile([P, D_OUT], F32, tag="h", name="h_tile", bufs=4)
             nc.sync.dma_start(out=h_of[n][:], in_=h_view[:, n, :])
@@ -93,31 +95,29 @@ def tile_onebitlinear_v_kernel(
                 out=h_of[n][:], in_=h_of[n][:], func=ACT.Identity, bias=line_of[n][:, 2:3], scale=line_of[n][:, 0:1]
             )
 
-        def turn(n):
-            banks_of[n] = []
-            for c in range(PASSES):
-                bank = turned.tile([P, PACK, P], F32, tag="turned")
-                banks_of[n].append(bank)
-                for j in range(PACK):
-                    cols = slice((c * PACK + j) * P, (c * PACK + j + 1) * P)
-                    nc.tensor.matmul(
-                        out=bank[:, j, :], lhsT=gr_of[n][:, cols], rhs=identity[:], is_transpose=True,
-                        start=True, stop=False,
-                    )
-                    nc.tensor.matmul(
-                        out=bank[:, j, :], lhsT=h_of[n][:, cols], rhs=identity[:], is_transpose=True,
-                        start=False, stop=True,
-                    )
-
-        def scale_round(n):
-            grouped_of[n] = stage.tile([P, PASSES, P, PACK], BF16, tag="grouped", name="grouped", align_bytes=64)
-            for c in range(PASSES):
-                nc.vector.tensor_tensor(
-                    out=grouped_of[n][:, c, :, :],
-                    in0=banks_of[n][c][:].rearrange("p j t -> p t j"),
-                    in1=ocs_col[:, c * PACK : (c + 1) * PACK].unsqueeze(1).to_broadcast([P, P, PACK]),
-                    op=ALU.mult,
+        def turn(n, c):
+            bank = turned.tile([P, PACK, P], F32, tag="turned")
+            banks_of[n, c] = bank
+            for j in range(PACK):
+                cols = slice((c * PACK + j) * P, (c * PACK + j + 1) * P)
+                nc.tensor.matmul(
+                    out=bank[:, j, :], lhsT=gr_of[n][:, cols], rhs=identity[:], is_transpose=True,
+                    start=True, stop=False,
                 )
+                nc.tensor.matmul(
+                    out=bank[:, j, :], lhsT=h_of[n][:, cols], rhs=identity[:], is_transpose=True,
+                    start=False, stop=True,
+                )
+
+        def scale_round(n, c):
+            if c == 0:
+                grouped_of[n] = stage.tile([P, PASSES, P, PACK], BF16, tag="grouped", name="grouped", align_bytes=64)
+            nc.vector.tensor_tensor(
+                out=grouped_of[n][:, c, :, :],
+                in0=banks_of[n, c][:].rearrange("p j t -> p t j"),
+                in1=ocs_col[:, c * PACK : (c + 1) * PACK].unsqueeze(1).to_broadcast([P, P, PACK]),
+                op=ALU.mult,
+            )
 
         def quantise_rows(n):
             nc.vector.quantize_mx(
@@ -171,18 +171,20 @@ def tile_onebitlinear_v_kernel(
                 )
 
         def times_x(n, chunk):
-            product_of[n, chunk] = stage.tile([P, N_TILE], F32, tag="product", name="product", bufs=7)
-            nc.vector.tensor_tensor(
-                out=product_of[n, chunk][:], in0=acc_of[n, chunk][:],
-                in1=x_all[:, n, chunk * N_TILE : (chunk + 1) * N_TILE], op=ALU.mult,
-            )
+            cols = slice(chunk * N_TILE, (chunk + 1) * N_TILE)
+            if n == 0:
+                nc.vector.tensor_tensor(out=running[:, cols], in0=acc_of[n, chunk][:], in1=x_all[:, n, cols], op=ALU.mult)
+            else:
+                product = stage.tile([P, N_TILE], F32, tag="product", bufs=4)
+                nc.vector.tensor_tensor(out=product[:], in0=acc_of[n, chunk][:], in1=x_all[:, n, cols], op=ALU.mult)
+                nc.gpsimd.tensor_tensor(out=running[:, cols], in0=running[:, cols], in1=product[:], op=ALU.add)
 
-        def add_tokens(n, chunk):
+        def add_tokens(chunk):
             for b in range(PACK):
                 col = chunk * PACK + b
                 nc.tensor.matmul(
-                    out=column_sums[:, n, col : col + 1], lhsT=product_of[n, chunk][:, b * P : (b + 1) * P],
-                    rhs=ones[:], start=True, stop=True,
+                    out=column_sums[:, col : col + 1], lhsT=running[:, col * P : (col + 1) * P], rhs=ones[:],
+                    start=True, stop=True,
                 )
 
         def cells_ready_after(s):
@@ -231,42 +233,45 @@ def tile_onebitlinear_v_kernel(
             row_sums(n)
             straight_line(n)
 
-        turn(0)
+        units = [(n, c) for n in range(TILES) for c in range(PASSES)]
+        for n, c in units[:TURN_LEAD]:
+            turn(n, c)
 
-        for s in range(TILES):
+        for s in range(TILES + 1):
             later = s + AHEAD
+            cells = cells_ready_after(s - 1)
             if later + 1 < TILES:
                 load_rows(later + 1)
-            load_x(s)
+            if s < TILES:
+                load_x(s)
             if 2 * s + 1 < W_LOADS:
                 weight_pair(2 * s + 1)
             if later < TILES:
                 scaled_gradient(later)
-                row_sums(later)
-                straight_line(later)
-            if 2 * s + 2 < W_LOADS:
-                weight_pair(2 * s + 2)
-            scale_round(s)
+            for i in range(max(PASSES, len(cells))):
+                if i == 2 and later < TILES:
+                    row_sums(later)
+                    straight_line(later)
+                    if 2 * s + 2 < W_LOADS:
+                        weight_pair(2 * s + 2)
+                if i < len(cells):
+                    multiply(*cells[i])
+                ahead = s * PASSES + i + TURN_LEAD
+                if i < PASSES and ahead < len(units):
+                    turn(*units[ahead])
+                if i < PASSES and s < TILES:
+                    scale_round(s, i)
+                if i < len(cells):
+                    times_x(*cells[i])
             if s < CHUNKS:
                 for c in range(PASSES):
                     quantise_weights(s, c)
-            quantise_rows(s)
-            for n, chunk in cells_ready_after(s - 1):
-                times_x(n, chunk)
-            if s + 1 < TILES:
-                turn(s + 1)
-            for n, chunk in cells_ready_after(s - 1):
-                add_tokens(n, chunk)
-            for n, chunk in cells_ready_after(s):
-                multiply(n, chunk)
-        for n, chunk in cells_ready_after(TILES - 1):
-            times_x(n, chunk)
-            add_tokens(n, chunk)
+            if s < TILES:
+                quantise_rows(s)
+        for chunk in range(CHUNKS):
+            add_tokens(chunk)
 
-        nc.vector.tensor_reduce(
-            out=out_square[:, 0 : CHUNKS * PACK], in_=column_sums[:].rearrange("p n c -> p c n"),
-            axis=mybir.AxisListType.X, op=ALU.add,
-        )
+        nc.vector.tensor_copy(out=out_square[:, 0 : CHUNKS * PACK], in_=column_sums[:])
         out_turned = turned.tile([P, PACK, P], F32, tag="turned")
         nc.tensor.transpose(out_turned[:, 0, :], out_square[:], identity[:])
         result = keep.tile([P, P], F32)

@@ -23,8 +23,7 @@ BLOCKS = D_OUT // P
 N_TILE = 512
 CHUNKS = D_IN // N_TILE
 W_LOADS = 2 * CHUNKS
-AHEAD = 2
-TURN_LEAD = 2
+ACC_BANKS = 3
 
 FLOPS = 2 * TOKENS * D_IN * D_OUT
 
@@ -39,7 +38,7 @@ def tile_onebitlinear_v_kernel(
         small = stack.enter_context(tc.tile_pool(name="small", bufs=4))
         stage = stack.enter_context(tc.tile_pool(name="stage", bufs=2))
         turned = stack.enter_context(tc.psum_pool(name="turned", bufs=4))
-        banks = stack.enter_context(tc.psum_pool(name="banks", bufs=3))
+        banks = stack.enter_context(tc.psum_pool(name="banks", bufs=ACC_BANKS))
         total = stack.enter_context(tc.psum_pool(name="total", bufs=1))
         stack.enter_context(tc.manual_schedule())
 
@@ -55,44 +54,40 @@ def tile_onebitlinear_v_kernel(
         dm_scales = keep.tile([P, TILES, PASSES, P], U8, align_bytes=64)
         column_sums = total.tile([P, CHUNKS * PACK], F32)
         running = keep.tile([P, D_IN], F32)
-        g_of, h_of, gr_of, sums_of, line_of, banks_of, grouped_of = {}, {}, {}, {}, {}, {}, {}
+        g_of, h_of, gr_of, sums_of, banks_of, grouped_of = {}, {}, {}, {}, {}, {}
         raw_of, signs_of, acc_of = {}, {}, {}
 
         def load_rows(n):
             g_of[n] = rows.tile([P, D_OUT], BF16, tag="g", name="g_tile", bufs=2)
             nc.sync.dma_start(out=g_of[n][:], in_=g_view[:, n, :])
-            h_of[n] = rows.tile([P, D_OUT], F32, tag="h", name="h_tile", bufs=4)
+            h_of[n] = rows.tile([P, D_OUT], F32, tag="h", name="h_tile")
             nc.sync.dma_start(out=h_of[n][:], in_=h_view[:, n, :])
 
         def load_x(n):
             nc.sync.dma_start(out=x_all[:, n, :], in_=x_view[:, n, :])
 
-        def scaled_gradient(n):
+        def row_sums(n):
             sums_of[n] = small.tile([P, 2], F32, tag="sums", name="sums")
             gr_of[n] = rows.tile([P, D_OUT], F32, tag="gr", name="gr")
             nc.vector.scalar_tensor_tensor(
                 out=gr_of[n][:], in0=g_of[n][:], scalar=rstd_sb[:, n : n + 1], in1=gamma_all[:],
                 op0=ALU.mult, op1=ALU.mult, accum_out=sums_of[n][:, 0:1],
             )
-
-        def row_sums(n):
             unread = stage.tile([P, D_OUT], F32, tag="unread", bufs=1)
             nc.vector.scalar_tensor_tensor(
                 out=unread[:], in0=h_of[n][:], scalar=mu_sb[:, n : n + 1], in1=gr_of[n][:],
                 op0=ALU.subtract, op1=ALU.mult, accum_out=sums_of[n][:, 1:2],
             )
-            line_of[n] = small.tile([P, 3], F32, tag="line", name="line")
-            nc.vector.tensor_scalar(
-                out=line_of[n][:, 0:2], in0=slope_of[:, n, :], scalar1=sums_of[n][:, 1:2], scalar2=None, op0=ALU.mult
-            )
-            nc.vector.scalar_tensor_tensor(
-                out=line_of[n][:, 2:3], in0=sums_of[n][:, 0:1], scalar=-1.0 / D_OUT, in1=line_of[n][:, 1:2],
-                op0=ALU.mult, op1=ALU.add,
-            )
 
         def straight_line(n):
+            line = small.tile([P, 3], F32, tag="line")
+            nc.scalar.activation(out=line[:, 0:1], in_=sums_of[n][:, 0:1], func=ACT.Copy, scale=-1.0 / D_OUT)
+            nc.scalar.activation(out=line[:, 1:2], in_=sums_of[n][:, 1:2], func=ACT.Copy, scale=slope_of[:, n, 0:1])
             nc.scalar.activation(
-                out=h_of[n][:], in_=h_of[n][:], func=ACT.Identity, bias=line_of[n][:, 2:3], scale=line_of[n][:, 0:1]
+                out=line[:, 2:3], in_=sums_of[n][:, 1:2], func=ACT.Identity, scale=slope_of[:, n, 1:2], bias=line[:, 0:1]
+            )
+            nc.scalar.activation(
+                out=h_of[n][:], in_=h_of[n][:], func=ACT.Identity, scale=line[:, 1:2], bias=line[:, 2:3]
             )
 
         def turn(n, c):
@@ -128,33 +123,30 @@ def tile_onebitlinear_v_kernel(
 
         def load_weights(load):
             chunk, half = divmod(load, 2)
-            raw_of[load] = stage.tile([P, 2 * PACK, N_TILE], BF16, tag="raw", name="raw")
+            raw_of[load] = stage.tile([P, 2, PACK, N_TILE], BF16, tag="raw", name="raw")
             nc.scalar.dma_start(
-                out=raw_of[load][:],
+                out=raw_of[load][:].rearrange("p k j i -> p (k j) i"),
                 in_=w_view[:, half * 2 * PACK : (half + 1) * 2 * PACK, chunk * N_TILE : (chunk + 1) * N_TILE],
             )
 
-        def weight_signs(chunk, c):
-            signs_of[chunk, c] = stage.tile([P, N_TILE, PACK], BF16, tag="signs", name="signs", bufs=4, align_bytes=64)
-            k = c % 2
-            nc.scalar.activation(
-                out=signs_of[chunk, c][:].rearrange("p (u i) j -> p u j i", i=4),
-                in_=raw_of[2 * chunk + c // 2][:, k * PACK : (k + 1) * PACK, :].rearrange("p j (u i) -> p u j i", i=4),
-                func=ACT.Sign, scale=2.0**120, bias=2.0**-20,
-            )
-
-        def weight_pair(load):
-            chunk, half = divmod(load, 2)
-            weight_signs(chunk, 2 * half)
-            weight_signs(chunk, 2 * half + 1)
+        def weight_signs(load):
+            signs_of[load] = stage.tile([P, 2, N_TILE, PACK], BF16, tag="signs", name="signs", align_bytes=64)
+            for k in range(2):
+                nc.scalar.activation(
+                    out=signs_of[load][:, k, :, :].rearrange("p (u i) j -> p u j i", i=4),
+                    in_=raw_of[load][:, k, :, :].rearrange("p j (u i) -> p u j i", i=4),
+                    func=ACT.Sign, scale=2.0**120, bias=2.0**-20,
+                )
             if load + 2 < W_LOADS:
                 load_weights(load + 2)
 
-        def quantise_weights(chunk, c):
+        def quantise_weights(load):
+            chunk, half = divmod(load, 2)
+            passes = slice(2 * half, 2 * half + 2)
             nc.vector.quantize_mx(
-                out=w_codes[:, chunk, c, :].bitcast(E4M3_X4),
-                scales=w_scales[:, chunk, c, :],
-                in_=signs_of[chunk, c][:].rearrange("p w j -> p (w j)"),
+                out=w_codes[:, chunk, passes, :].rearrange("p c i -> p (c i)").bitcast(E4M3_X4),
+                scales=w_scales[:, chunk, passes, :].rearrange("p c i -> p (c i)"),
+                in_=signs_of[load][:].rearrange("p k i j -> p (k i j)"),
             )
 
         def multiply(n, chunk):
@@ -202,7 +194,6 @@ def tile_onebitlinear_v_kernel(
         load_weights(0)
         load_rows(1)
         load_weights(1)
-        load_rows(2)
 
         identity = keep.tile([P, P], F32)
         make_identity(nc, identity[:])
@@ -227,45 +218,47 @@ def tile_onebitlinear_v_kernel(
         ocs_col = keep.tile([P, BLOCKS], F32)
         nc.vector.tensor_copy(out=ocs_col[:], in_=ocs_turned[:, 0, 0:BLOCKS])
 
-        weight_pair(0)
-        for n in range(AHEAD):
-            scaled_gradient(n)
-            row_sums(n)
-            straight_line(n)
-
-        units = [(n, c) for n in range(TILES) for c in range(PASSES)]
-        for n, c in units[:TURN_LEAD]:
-            turn(n, c)
+        weight_signs(0)
+        row_sums(0)
+        straight_line(0)
+        turn(0, 0)
 
         for s in range(TILES + 1):
-            later = s + AHEAD
             cells = cells_ready_after(s - 1)
-            if later + 1 < TILES:
-                load_rows(later + 1)
+            if s + 2 < TILES:
+                load_rows(s + 2)
             if s < TILES:
                 load_x(s)
             if 2 * s + 1 < W_LOADS:
-                weight_pair(2 * s + 1)
-            if later < TILES:
-                scaled_gradient(later)
-            for i in range(max(PASSES, len(cells))):
-                if i == 2 and later < TILES:
-                    row_sums(later)
-                    straight_line(later)
-                    if 2 * s + 2 < W_LOADS:
-                        weight_pair(2 * s + 2)
-                if i < len(cells):
-                    multiply(*cells[i])
-                ahead = s * PASSES + i + TURN_LEAD
-                if i < PASSES and ahead < len(units):
-                    turn(*units[ahead])
-                if i < PASSES and s < TILES:
-                    scale_round(s, i)
-                if i < len(cells):
-                    times_x(*cells[i])
+                weight_signs(2 * s + 1)
+            if s + 1 < TILES:
+                row_sums(s + 1)
+                straight_line(s + 1)
             if s < CHUNKS:
-                for c in range(PASSES):
-                    quantise_weights(s, c)
+                quantise_weights(2 * s)
+            if 2 * s + 2 < W_LOADS:
+                weight_signs(2 * s + 2)
+            first, rest = cells[:ACC_BANKS], cells[ACC_BANKS:]
+            for n, chunk in first:
+                multiply(n, chunk)
+            if s < TILES:
+                for c in range(1, PASSES):
+                    turn(s, c)
+            for n, chunk in first:
+                times_x(n, chunk)
+            if s < TILES:
+                scale_round(s, 0)
+                scale_round(s, 1)
+            for n, chunk in rest:
+                multiply(n, chunk)
+                times_x(n, chunk)
+            if s + 1 < TILES:
+                turn(s + 1, 0)
+            if s < TILES:
+                scale_round(s, 2)
+                scale_round(s, 3)
+            if s < CHUNKS:
+                quantise_weights(2 * s + 1)
             if s < TILES:
                 quantise_rows(s)
         for chunk in range(CHUNKS):

@@ -11,6 +11,7 @@ E4M3_X4 = mybir.dt.float8_e4m3fn_x4
 E5M2_X4 = mybir.dt.float8_e5m2_x4
 ALU = mybir.AluOpType
 ACT = mybir.ActivationFunctionType
+AX = mybir.AxisListType
 
 P = 128
 PACK = 4
@@ -23,7 +24,11 @@ BLOCKS = D_OUT // P
 N_TILE = 512
 CHUNKS = D_IN // N_TILE
 W_LOADS = 2 * CHUNKS
-ACC_BANKS = 3
+W_UNITS = 2 * W_LOADS
+HALF = D_OUT // 2
+SLOTS = 5
+SIGNS_A_STEP = 3
+AHEAD = 2
 
 FLOPS = 2 * TOKENS * D_IN * D_OUT
 
@@ -37,8 +42,8 @@ def tile_onebitlinear_v_kernel(
         rows = stack.enter_context(tc.tile_pool(name="rows", bufs=3))
         small = stack.enter_context(tc.tile_pool(name="small", bufs=4))
         stage = stack.enter_context(tc.tile_pool(name="stage", bufs=2))
-        turned = stack.enter_context(tc.psum_pool(name="turned", bufs=4))
-        banks = stack.enter_context(tc.psum_pool(name="banks", bufs=ACC_BANKS))
+        turned = stack.enter_context(tc.psum_pool(name="turned", bufs=2))
+        banks = stack.enter_context(tc.psum_pool(name="banks", bufs=2))
         total = stack.enter_context(tc.psum_pool(name="total", bufs=1))
         stack.enter_context(tc.manual_schedule())
 
@@ -52,39 +57,46 @@ def tile_onebitlinear_v_kernel(
         w_scales = keep.tile([P, CHUNKS, PASSES, N_TILE], U8, align_bytes=64)
         dm_codes = keep.tile([P, TILES, PASSES, P], U32, align_bytes=64)
         dm_scales = keep.tile([P, TILES, PASSES, P], U8, align_bytes=64)
-        column_sums = total.tile([P, CHUNKS * PACK], F32)
-        running = keep.tile([P, D_IN], F32)
+        token_sums = [total.tile([P, PACK, P], F32, tag="sums%d" % chunk, name="token_sums") for chunk in range(CHUNKS)]
         g_of, h_of, gr_of, sums_of, banks_of, grouped_of = {}, {}, {}, {}, {}, {}
-        raw_of, signs_of, acc_of = {}, {}, {}
+        raw_of, signs_of, acc_of, product_of = {}, {}, {}, {}
+        added = [0] * CHUNKS
 
         def load_rows(n):
-            g_of[n] = rows.tile([P, D_OUT], BF16, tag="g", name="g_tile", bufs=2)
+            g_of[n] = rows.tile([P, D_OUT], BF16, tag="g", name="g_tile")
             nc.sync.dma_start(out=g_of[n][:], in_=g_view[:, n, :])
-            h_of[n] = rows.tile([P, D_OUT], F32, tag="h", name="h_tile")
+            h_of[n] = rows.tile([P, D_OUT], F32, tag="h", name="h_tile", bufs=4)
             nc.sync.dma_start(out=h_of[n][:], in_=h_view[:, n, :])
 
         def load_x(n):
             nc.sync.dma_start(out=x_all[:, n, :], in_=x_view[:, n, :])
 
-        def row_sums(n):
-            sums_of[n] = small.tile([P, 2], F32, tag="sums", name="sums")
-            gr_of[n] = rows.tile([P, D_OUT], F32, tag="gr", name="gr")
-            nc.vector.scalar_tensor_tensor(
-                out=gr_of[n][:], in0=g_of[n][:], scalar=rstd_sb[:, n : n + 1], in1=gamma_all[:],
-                op0=ALU.mult, op1=ALU.mult, accum_out=sums_of[n][:, 0:1],
-            )
-            unread = stage.tile([P, D_OUT], F32, tag="unread", bufs=1)
-            nc.vector.scalar_tensor_tensor(
-                out=unread[:], in0=h_of[n][:], scalar=mu_sb[:, n : n + 1], in1=gr_of[n][:],
-                op0=ALU.subtract, op1=ALU.mult, accum_out=sums_of[n][:, 1:2],
-            )
+        def row_piece(n, piece):
+            half = piece % 2
+            cols = slice(half * HALF, (half + 1) * HALF)
+            if piece == 0:
+                sums_of[n] = small.tile([P, 4], F32, tag="sums", name="sums")
+                gr_of[n] = rows.tile([P, D_OUT], F32, tag="gr", name="gr")
+            if piece < 2:
+                nc.vector.scalar_tensor_tensor(
+                    out=gr_of[n][:, cols], in0=g_of[n][:, cols], scalar=rstd_sb[:, n : n + 1], in1=gamma_all[:, cols],
+                    op0=ALU.mult, op1=ALU.mult, accum_out=sums_of[n][:, piece : piece + 1],
+                )
+            else:
+                unread = stage.tile([P, HALF], F32, tag="unread", bufs=1)
+                nc.vector.scalar_tensor_tensor(
+                    out=unread[:], in0=h_of[n][:, cols], scalar=mu_sb[:, n : n + 1], in1=gr_of[n][:, cols],
+                    op0=ALU.subtract, op1=ALU.mult, accum_out=sums_of[n][:, piece : piece + 1],
+                )
 
         def straight_line(n):
+            both = small.tile([P, 2], F32, tag="both")
+            nc.vector.tensor_tensor(out=both[:], in0=sums_of[n][:, 0:4:2], in1=sums_of[n][:, 1:4:2], op=ALU.add)
             line = small.tile([P, 3], F32, tag="line")
-            nc.scalar.activation(out=line[:, 0:1], in_=sums_of[n][:, 0:1], func=ACT.Copy, scale=-1.0 / D_OUT)
-            nc.scalar.activation(out=line[:, 1:2], in_=sums_of[n][:, 1:2], func=ACT.Copy, scale=slope_of[:, n, 0:1])
+            nc.scalar.activation(out=line[:, 0:1], in_=both[:, 0:1], func=ACT.Copy, scale=-1.0 / D_OUT)
+            nc.scalar.activation(out=line[:, 1:2], in_=both[:, 1:2], func=ACT.Copy, scale=slope_of[:, n, 0:1])
             nc.scalar.activation(
-                out=line[:, 2:3], in_=sums_of[n][:, 1:2], func=ACT.Identity, scale=slope_of[:, n, 1:2], bias=line[:, 0:1]
+                out=line[:, 2:3], in_=both[:, 1:2], func=ACT.Identity, scale=slope_of[:, n, 1:2], bias=line[:, 0:1]
             )
             nc.scalar.activation(
                 out=h_of[n][:], in_=h_of[n][:], func=ACT.Identity, scale=line[:, 1:2], bias=line[:, 2:3]
@@ -129,15 +141,16 @@ def tile_onebitlinear_v_kernel(
                 in_=w_view[:, half * 2 * PACK : (half + 1) * 2 * PACK, chunk * N_TILE : (chunk + 1) * N_TILE],
             )
 
-        def weight_signs(load):
-            signs_of[load] = stage.tile([P, 2, N_TILE, PACK], BF16, tag="signs", name="signs", align_bytes=64)
-            for k in range(2):
-                nc.scalar.activation(
-                    out=signs_of[load][:, k, :, :].rearrange("p (u i) j -> p u j i", i=4),
-                    in_=raw_of[load][:, k, :, :].rearrange("p j (u i) -> p u j i", i=4),
-                    func=ACT.Sign, scale=2.0**120, bias=2.0**-20,
-                )
-            if load + 2 < W_LOADS:
+        def weight_signs(unit):
+            load, k = divmod(unit, 2)
+            if k == 0:
+                signs_of[load] = stage.tile([P, 2, N_TILE, PACK], BF16, tag="signs", name="signs", align_bytes=64)
+            nc.scalar.activation(
+                out=signs_of[load][:, k, :, :].rearrange("p (u i) j -> p u j i", i=4),
+                in_=raw_of[load][:, k, :, :].rearrange("p j (u i) -> p u j i", i=4),
+                func=ACT.Sign, scale=2.0**120, bias=2.0**-20,
+            )
+            if k == 1 and load + 2 < W_LOADS:
                 load_weights(load + 2)
 
         def quantise_weights(load):
@@ -164,23 +177,16 @@ def tile_onebitlinear_v_kernel(
 
         def times_x(n, chunk):
             cols = slice(chunk * N_TILE, (chunk + 1) * N_TILE)
-            if n == 0:
-                nc.vector.tensor_tensor(out=running[:, cols], in0=acc_of[n, chunk][:], in1=x_all[:, n, cols], op=ALU.mult)
-            else:
-                product = stage.tile([P, N_TILE], F32, tag="product", bufs=4)
-                nc.vector.tensor_tensor(out=product[:], in0=acc_of[n, chunk][:], in1=x_all[:, n, cols], op=ALU.mult)
-                nc.gpsimd.tensor_tensor(out=running[:, cols], in0=running[:, cols], in1=product[:], op=ALU.add)
+            product_of[n, chunk] = stage.tile([P, N_TILE], F32, tag="product", name="product", bufs=4)
+            nc.vector.tensor_tensor(out=product_of[n, chunk][:], in0=acc_of[n, chunk][:], in1=x_all[:, n, cols], op=ALU.mult)
 
-        def add_tokens(chunk):
+        def add_tokens(n, chunk):
             for b in range(PACK):
-                col = chunk * PACK + b
+                added[chunk] += 1
                 nc.tensor.matmul(
-                    out=column_sums[:, col : col + 1], lhsT=running[:, col * P : (col + 1) * P], rhs=ones[:],
-                    start=True, stop=True,
+                    out=token_sums[chunk][:, b, :], lhsT=product_of[n, chunk][:, b * P : (b + 1) * P], rhs=identity[:],
+                    is_transpose=True, start=(added[chunk] == 1), stop=(added[chunk] == TILES * PACK),
                 )
-
-        def cells_ready_after(s):
-            return [(n, chunk) for n in range(TILES) for chunk in range(CHUNKS) if max(n, chunk) == s]
 
         rstd_sb = keep.tile([P, TILES], F32)
         nc.sync.dma_start(out=rstd_sb[:], in_=rstd.rearrange("(p n) o -> p (n o)", n=TILES))
@@ -194,11 +200,10 @@ def tile_onebitlinear_v_kernel(
         load_weights(0)
         load_rows(1)
         load_weights(1)
+        load_rows(2)
 
         identity = keep.tile([P, P], F32)
         make_identity(nc, identity[:])
-        ones = keep.tile([P, 1], F32)
-        nc.vector.memset(ones[:], 1.0)
         ocs_square = keep.tile([P, P], F32)
         nc.vector.memset(ocs_square[:], 0.0)
         out_square = keep.tile([P, P], F32)
@@ -219,52 +224,66 @@ def tile_onebitlinear_v_kernel(
         nc.vector.tensor_copy(out=ocs_col[:], in_=ocs_turned[:, 0, 0:BLOCKS])
 
         weight_signs(0)
-        row_sums(0)
-        straight_line(0)
-        turn(0, 0)
+        weight_signs(1)
+        for n in range(AHEAD):
+            for piece in range(4):
+                row_piece(n, piece)
+            straight_line(n)
+            if n == 0:
+                turn(0, 0)
+                turn(0, 1)
 
-        for s in range(TILES + 1):
-            cells = cells_ready_after(s - 1)
-            if s + 2 < TILES:
-                load_rows(s + 2)
+        ready = []
+        counts = {"started": 0, "finished": 0, "unit": 2, "load": 0, "slot": 0}
+        signed_at = {0: 0}
+        tiles_done, chunks_done = [], []
+        for s in range(TILES + 3):
+            if s + AHEAD + 1 < TILES:
+                load_rows(s + AHEAD + 1)
             if s < TILES:
                 load_x(s)
-            if 2 * s + 1 < W_LOADS:
-                weight_signs(2 * s + 1)
-            if s + 1 < TILES:
-                row_sums(s + 1)
-                straight_line(s + 1)
-            if s < CHUNKS:
-                quantise_weights(2 * s)
-            if 2 * s + 2 < W_LOADS:
-                weight_signs(2 * s + 2)
-            first, rest = cells[:ACC_BANKS], cells[ACC_BANKS:]
-            for n, chunk in first:
-                multiply(n, chunk)
-            if s < TILES:
-                for c in range(1, PASSES):
-                    turn(s, c)
-            for n, chunk in first:
-                times_x(n, chunk)
-            if s < TILES:
-                scale_round(s, 0)
-                scale_round(s, 1)
-            for n, chunk in rest:
-                multiply(n, chunk)
-                times_x(n, chunk)
-            if s + 1 < TILES:
-                turn(s + 1, 0)
-            if s < TILES:
-                scale_round(s, 2)
-                scale_round(s, 3)
-            if s < CHUNKS:
-                quantise_weights(2 * s + 1)
-            if s < TILES:
-                quantise_rows(s)
-        for chunk in range(CHUNKS):
-            add_tokens(chunk)
+            for i in range(SLOTS):
+                counts["slot"] += 1
+                if i < SIGNS_A_STEP and counts["unit"] < W_UNITS:
+                    weight_signs(counts["unit"])
+                    if counts["unit"] % 2 == 1:
+                        signed_at[counts["unit"] // 2] = counts["slot"]
+                    counts["unit"] += 1
+                if s + AHEAD < TILES:
+                    if i < 4:
+                        row_piece(s + AHEAD, i)
+                    else:
+                        straight_line(s + AHEAD)
+                if counts["finished"] < counts["started"]:
+                    cell = ready[counts["finished"]]
+                    times_x(*cell)
+                    add_tokens(*cell)
+                    counts["finished"] += 1
+                while counts["started"] < len(ready) and counts["started"] - counts["finished"] < 2:
+                    multiply(*ready[counts["started"]])
+                    counts["started"] += 1
+                if s < TILES and i < PASSES:
+                    scale_round(s, i)
+                    n_next, c_next = divmod(s * PASSES + i + 2, PASSES)
+                    if n_next < TILES:
+                        turn(n_next, c_next)
+                load = counts["load"]
+                if load < W_LOADS and signed_at.get(load, counts["slot"]) + 2 <= counts["slot"]:
+                    quantise_weights(load)
+                    counts["load"] += 1
+                    if load % 2 == 1:
+                        chunks_done.append(load // 2)
+                        ready.extend([(n, load // 2) for n in tiles_done])
+                if s < TILES and i == SLOTS - 1:
+                    quantise_rows(s)
+                    tiles_done.append(s)
+                    ready.extend([(s, chunk) for chunk in chunks_done])
+        assert counts["finished"] == TILES * CHUNKS
 
-        nc.vector.tensor_copy(out=out_square[:, 0 : CHUNKS * PACK], in_=column_sums[:])
+        for chunk in range(CHUNKS):
+            nc.vector.tensor_reduce(
+                out=out_square[:, chunk * PACK : (chunk + 1) * PACK], in_=token_sums[chunk][:], op=ALU.add, axis=AX.X
+            )
         out_turned = turned.tile([P, PACK, P], F32, tag="turned")
         nc.tensor.transpose(out_turned[:, 0, :], out_square[:], identity[:])
         result = keep.tile([P, P], F32)

@@ -61,6 +61,9 @@ def tile_onebitlinear_v_kernel(
         g_of, h_of, gr_of, sums_of, banks_of, grouped_of = {}, {}, {}, {}, {}, {}
         raw_of, signs_of, acc_of, product_of = {}, {}, {}, {}
         added = [0] * CHUNKS
+        cells_done = [0] * CHUNKS
+        running = keep.tile([P, D_IN], F32)
+        running_begun, to_reduce, waiting, closing = [], [], [], []
 
         def load_rows(n):
             g_of[n] = rows.tile([P, D_OUT], BF16, tag="g", name="g_tile")
@@ -180,13 +183,38 @@ def tile_onebitlinear_v_kernel(
             product_of[n, chunk] = stage.tile([P, N_TILE], F32, tag="product", name="product", bufs=4)
             nc.vector.tensor_tensor(out=product_of[n, chunk][:], in0=acc_of[n, chunk][:], in1=x_all[:, n, cols], op=ALU.mult)
 
-        def add_tokens(n, chunk):
+        def add_tokens(chunk, product, last):
             for b in range(PACK):
                 added[chunk] += 1
                 nc.tensor.matmul(
-                    out=token_sums[chunk][:, b, :], lhsT=product_of[n, chunk][:, b * P : (b + 1) * P], rhs=identity[:],
-                    is_transpose=True, start=(added[chunk] == 1), stop=(added[chunk] == TILES * PACK),
+                    out=token_sums[chunk][:, b, :], lhsT=product[:, b * P : (b + 1) * P], rhs=identity[:],
+                    is_transpose=True, start=(added[chunk] == 1), stop=(last and b == PACK - 1),
                 )
+
+        def times_x_late(n, chunk):
+            cols = slice(chunk * N_TILE, (chunk + 1) * N_TILE)
+            if chunk not in running_begun:
+                running_begun.append(chunk)
+                nc.vector.tensor_tensor(out=running[:, cols], in0=acc_of[n, chunk][:], in1=x_all[:, n, cols], op=ALU.mult)
+                settle(chunk)
+            else:
+                times_x(n, chunk)
+                waiting.append((n, chunk))
+
+        def add_late(n, chunk):
+            cols = slice(chunk * N_TILE, (chunk + 1) * N_TILE)
+            nc.vector.tensor_tensor(out=running[:, cols], in0=running[:, cols], in1=product_of[n, chunk][:], op=ALU.add)
+            settle(chunk)
+
+        def settle(chunk):
+            cells_done[chunk] += 1
+            if cells_done[chunk] == TILES:
+                closing.append(chunk)
+
+        def reduce_chunk(chunk):
+            nc.vector.tensor_reduce(
+                out=out_square[:, chunk * PACK : (chunk + 1) * PACK], in_=token_sums[chunk][:], op=ALU.add, axis=AX.X
+            )
 
         rstd_sb = keep.tile([P, TILES], F32)
         nc.sync.dma_start(out=rstd_sb[:], in_=rstd.rearrange("(p n) o -> p (n o)", n=TILES))
@@ -234,7 +262,7 @@ def tile_onebitlinear_v_kernel(
                 turn(0, 1)
 
         ready = []
-        counts = {"started": 0, "finished": 0, "unit": 2, "load": 0, "slot": 0}
+        counts = {"started": 0, "finished": 0, "unit": 2, "load": 0, "slot": 0, "summed": 0}
         signed_at = {0: 0}
         tiles_done, chunks_done = [], []
         for s in range(TILES + 3):
@@ -256,12 +284,27 @@ def tile_onebitlinear_v_kernel(
                         straight_line(s + AHEAD)
                 if counts["finished"] < counts["started"]:
                     cell = ready[counts["finished"]]
-                    times_x(*cell)
-                    add_tokens(*cell)
+                    if s + AHEAD < TILES:
+                        times_x(*cell)
+                        add_tokens(cell[1], product_of[cell], False)
+                        settle(cell[1])
+                    else:
+                        times_x_late(*cell)
                     counts["finished"] += 1
+                behind = 1 if counts["finished"] < TILES * CHUNKS else 0
+                while counts["summed"] < len(waiting) - behind:
+                    add_late(*waiting[counts["summed"]])
+                    counts["summed"] += 1
+                for chunk in to_reduce:
+                    reduce_chunk(chunk)
+                to_reduce.clear()
                 while counts["started"] < len(ready) and counts["started"] - counts["finished"] < 2:
                     multiply(*ready[counts["started"]])
                     counts["started"] += 1
+                for chunk in closing:
+                    add_tokens(chunk, running[:, chunk * N_TILE : (chunk + 1) * N_TILE], True)
+                    to_reduce.append(chunk)
+                closing.clear()
                 if s < TILES and i < PASSES:
                     scale_round(s, i)
                     n_next, c_next = divmod(s * PASSES + i + 2, PASSES)
@@ -280,10 +323,7 @@ def tile_onebitlinear_v_kernel(
                     ready.extend([(s, chunk) for chunk in chunks_done])
         assert counts["finished"] == TILES * CHUNKS
 
-        for chunk in range(CHUNKS):
-            nc.vector.tensor_reduce(
-                out=out_square[:, chunk * PACK : (chunk + 1) * PACK], in_=token_sums[chunk][:], op=ALU.add, axis=AX.X
-            )
+        assert not to_reduce
         out_turned = turned.tile([P, PACK, P], F32, tag="turned")
         nc.tensor.transpose(out_turned[:, 0, :], out_square[:], identity[:])
         result = keep.tile([P, P], F32)

@@ -31,6 +31,12 @@ SIGNS_A_STEP = 3
 AHEAD = 2
 
 FLOPS = 2 * TOKENS * D_IN * D_OUT
+TINY = "s"
+HEAD = "new"
+LATE_FROM = 5
+LATE_G = 0
+LAST_T = 1
+SIGNS_A_STEP = 3
 
 
 def tile_onebitlinear_v_kernel(
@@ -63,44 +69,54 @@ def tile_onebitlinear_v_kernel(
         added = [0] * CHUNKS
         cells_done = [0] * CHUNKS
         running = keep.tile([P, D_IN], F32)
-        running_begun, to_reduce, waiting, closing = [], [], [], []
+        running_begun, to_reduce, waiting, closing, to_reduce_next = [], [], [], [], []
 
-        def load_rows(n):
+        def load_g(n):
             g_of[n] = rows.tile([P, D_OUT], BF16, tag="g", name="g_tile")
             nc.sync.dma_start(out=g_of[n][:], in_=g_view[:, n, :])
+
+        def load_h(n):
             h_of[n] = rows.tile([P, D_OUT], F32, tag="h", name="h_tile", bufs=4)
             nc.sync.dma_start(out=h_of[n][:], in_=h_view[:, n, :])
+
+        def load_rows(n):
+            load_g(n)
+            load_h(n)
 
         def load_x(n):
             nc.sync.dma_start(out=x_all[:, n, :], in_=x_view[:, n, :])
 
         def row_piece(n, piece):
-            half = piece % 2
-            cols = slice(half * HALF, (half + 1) * HALF)
             if piece == 0:
-                sums_of[n] = small.tile([P, 4], F32, tag="sums", name="sums")
+                sums_of[n] = small.tile([P, 2], F32, tag="sums", name="sums")
                 gr_of[n] = rows.tile([P, D_OUT], F32, tag="gr", name="gr")
-            if piece < 2:
                 nc.vector.scalar_tensor_tensor(
-                    out=gr_of[n][:, cols], in0=g_of[n][:, cols], scalar=rstd_sb[:, n : n + 1], in1=gamma_all[:, cols],
-                    op0=ALU.mult, op1=ALU.mult, accum_out=sums_of[n][:, piece : piece + 1],
+                    out=gr_of[n][:], in0=g_of[n][:], scalar=rstd_sb[:, n : n + 1], in1=gamma_all[:],
+                    op0=ALU.mult, op1=ALU.mult, accum_out=sums_of[n][:, 0:1],
                 )
             else:
-                unread = stage.tile([P, HALF], F32, tag="unread", bufs=1)
+                unread = stage.tile([P, D_OUT], F32, tag="unread", bufs=1)
                 nc.vector.scalar_tensor_tensor(
-                    out=unread[:], in0=h_of[n][:, cols], scalar=mu_sb[:, n : n + 1], in1=gr_of[n][:, cols],
-                    op0=ALU.subtract, op1=ALU.mult, accum_out=sums_of[n][:, piece : piece + 1],
+                    out=unread[:], in0=h_of[n][:], scalar=mu_sb[:, n : n + 1], in1=gr_of[n][:],
+                    op0=ALU.subtract, op1=ALU.mult, accum_out=sums_of[n][:, 1:2],
                 )
 
         def straight_line(n):
-            both = small.tile([P, 2], F32, tag="both")
-            nc.vector.tensor_tensor(out=both[:], in0=sums_of[n][:, 0:4:2], in1=sums_of[n][:, 1:4:2], op=ALU.add)
+            both = sums_of[n]
             line = small.tile([P, 3], F32, tag="line")
-            nc.scalar.activation(out=line[:, 0:1], in_=both[:, 0:1], func=ACT.Copy, scale=-1.0 / D_OUT)
-            nc.scalar.activation(out=line[:, 1:2], in_=both[:, 1:2], func=ACT.Copy, scale=slope_of[:, n, 0:1])
-            nc.scalar.activation(
-                out=line[:, 2:3], in_=both[:, 1:2], func=ACT.Identity, scale=slope_of[:, n, 1:2], bias=line[:, 0:1]
-            )
+            te = {'v': nc.vector, 'g': nc.gpsimd}.get(TINY)
+            if te:
+                te.tensor_scalar(out=line[:, 0:1], in0=both[:, 0:1], scalar1=-1.0 / D_OUT, scalar2=None, op0=ALU.mult)
+                te.tensor_scalar(out=line[:, 1:2], in0=both[:, 1:2], scalar1=slope_of[:, n, 0:1], scalar2=None, op0=ALU.mult)
+                te.tensor_scalar(
+                    out=line[:, 2:3], in0=both[:, 1:2], scalar1=slope_of[:, n, 1:2], scalar2=line[:, 0:1], op0=ALU.mult, op1=ALU.add
+                )
+            else:
+                nc.scalar.activation(out=line[:, 0:1], in_=both[:, 0:1], func=ACT.Copy, scale=-1.0 / D_OUT)
+                nc.scalar.activation(out=line[:, 1:2], in_=both[:, 1:2], func=ACT.Copy, scale=slope_of[:, n, 0:1])
+                nc.scalar.activation(
+                    out=line[:, 2:3], in_=both[:, 1:2], func=ACT.Identity, scale=slope_of[:, n, 1:2], bias=line[:, 0:1]
+                )
             nc.scalar.activation(
                 out=h_of[n][:], in_=h_of[n][:], func=ACT.Identity, scale=line[:, 1:2], bias=line[:, 2:3]
             )
@@ -136,10 +152,10 @@ def tile_onebitlinear_v_kernel(
                 in_=grouped_of[n][:].rearrange("p c t j -> p (c t j)"),
             )
 
-        def load_weights(load):
+        def load_weights(load, queue=None):
             chunk, half = divmod(load, 2)
             raw_of[load] = stage.tile([P, 2, PACK, N_TILE], BF16, tag="raw", name="raw")
-            nc.scalar.dma_start(
+            (queue or nc.scalar).dma_start(
                 out=raw_of[load][:].rearrange("p k j i -> p (k j) i"),
                 in_=w_view[:, half * 2 * PACK : (half + 1) * 2 * PACK, chunk * N_TILE : (chunk + 1) * N_TILE],
             )
@@ -203,12 +219,12 @@ def tile_onebitlinear_v_kernel(
 
         def add_late(n, chunk):
             cols = slice(chunk * N_TILE, (chunk + 1) * N_TILE)
-            nc.vector.tensor_tensor(out=running[:, cols], in0=running[:, cols], in1=product_of[n, chunk][:], op=ALU.add)
+            (nc.gpsimd if LATE_G else nc.vector).tensor_tensor(out=running[:, cols], in0=running[:, cols], in1=product_of[n, chunk][:], op=ALU.add)
             settle(chunk)
 
         def settle(chunk):
             cells_done[chunk] += 1
-            if cells_done[chunk] == TILES:
+            if cells_done[chunk] == TILES - LAST_T:
                 closing.append(chunk)
 
         def reduce_chunk(chunk):
@@ -216,19 +232,37 @@ def tile_onebitlinear_v_kernel(
                 out=out_square[:, chunk * PACK : (chunk + 1) * PACK], in_=token_sums[chunk][:], op=ALU.add, axis=AX.X
             )
 
-        rstd_sb = keep.tile([P, TILES], F32)
-        nc.sync.dma_start(out=rstd_sb[:], in_=rstd.rearrange("(p n) o -> p (n o)", n=TILES))
-        mu_sb = keep.tile([P, TILES], F32)
-        nc.sync.dma_start(out=mu_sb[:], in_=mu.rearrange("(p n) o -> p (n o)", n=TILES))
-        gamma_all = keep.tile([P, D_OUT], BF16)
-        nc.scalar.dma_start(out=gamma_all[:], in_=ln_gamma.partition_broadcast(P))
-        ocs_rows = keep.tile([BLOCKS, P], BF16)
-        nc.sync.dma_start(out=ocs_rows[:], in_=out_channel_scale.rearrange("(b p) -> b p", p=P))
-        load_rows(0)
-        load_weights(0)
-        load_rows(1)
-        load_weights(1)
-        load_rows(2)
+        if HEAD == 'old':
+            rstd_sb = keep.tile([P, TILES], F32)
+            nc.sync.dma_start(out=rstd_sb[:], in_=rstd.rearrange("(p n) o -> p (n o)", n=TILES))
+            mu_sb = keep.tile([P, TILES], F32)
+            nc.sync.dma_start(out=mu_sb[:], in_=mu.rearrange("(p n) o -> p (n o)", n=TILES))
+            gamma_all = keep.tile([P, D_OUT], BF16)
+            nc.scalar.dma_start(out=gamma_all[:], in_=ln_gamma.partition_broadcast(P))
+            ocs_rows = keep.tile([BLOCKS, P], BF16)
+            nc.sync.dma_start(out=ocs_rows[:], in_=out_channel_scale.rearrange("(b p) -> b p", p=P))
+            load_rows(0)
+            load_weights(0)
+            load_rows(1)
+            load_weights(1)
+            load_rows(2)
+        else:
+            rstd_sb = keep.tile([P, TILES], F32)
+            mu_sb = keep.tile([P, TILES], F32)
+            gamma_all = keep.tile([P, D_OUT], BF16)
+            ocs_rows = keep.tile([BLOCKS, P], BF16)
+            nc.sync.dma_start(out=rstd_sb[:], in_=rstd.rearrange("(p n) o -> p (n o)", n=TILES))
+            load_g(0)
+            nc.sync.dma_start(out=gamma_all[:], in_=ln_gamma.partition_broadcast(P))
+            nc.sync.dma_start(out=mu_sb[:], in_=mu.rearrange("(p n) o -> p (n o)", n=TILES))
+            load_weights(0, nc.sync)
+            load_h(0)
+            nc.sync.dma_start(out=ocs_rows[:], in_=out_channel_scale.rearrange("(b p) -> b p", p=P))
+            load_g(1)
+            load_h(1)
+            load_weights(1, nc.sync)
+            load_g(2)
+            load_h(2)
 
         identity = keep.tile([P, P], F32)
         make_identity(nc, identity[:])
@@ -245,18 +279,23 @@ def tile_onebitlinear_v_kernel(
             out=slope_of[:, :, 1], in0=slope_of[:, :, 0], scalar=-1.0, in1=mu_sb[:], op0=ALU.mult, op1=ALU.mult
         )
 
-        nc.vector.tensor_copy(out=ocs_square[0:BLOCKS, :], in_=ocs_rows[:])
-        ocs_turned = turned.tile([P, PACK, P], F32, tag="turned")
-        nc.tensor.transpose(ocs_turned[:, 0, :], ocs_square[:], identity[:])
-        ocs_col = keep.tile([P, BLOCKS], F32)
-        nc.vector.tensor_copy(out=ocs_col[:], in_=ocs_turned[:, 0, 0:BLOCKS])
+        def prepare_ocs():
+            nc.vector.tensor_copy(out=ocs_square[0:BLOCKS, :], in_=ocs_rows[:])
+            ocs_turned = turned.tile([P, PACK, P], F32, tag="turned")
+            nc.tensor.transpose(ocs_turned[:, 0, :], ocs_square[:], identity[:])
+            nc.vector.tensor_copy(out=ocs_col[:], in_=ocs_turned[:, 0, 0:BLOCKS])
 
+        ocs_col = keep.tile([P, BLOCKS], F32)
+        if HEAD == 'old':
+            prepare_ocs()
         weight_signs(0)
         weight_signs(1)
         for n in range(AHEAD):
-            for piece in range(4):
+            for piece in range(2):
                 row_piece(n, piece)
             straight_line(n)
+            if n == 0 and HEAD != 'old':
+                prepare_ocs()
             if n == 0:
                 turn(0, 0)
                 turn(0, 1)
@@ -278,32 +317,42 @@ def tile_onebitlinear_v_kernel(
                         signed_at[counts["unit"] // 2] = counts["slot"]
                     counts["unit"] += 1
                 if s + AHEAD < TILES:
-                    if i < 4:
-                        row_piece(s + AHEAD, i)
-                    else:
+                    if i in (0, 2):
+                        row_piece(s + AHEAD, i // 2)
+                    elif i == 3:
                         straight_line(s + AHEAD)
+                due = len(waiting)
                 if counts["finished"] < counts["started"]:
                     cell = ready[counts["finished"]]
-                    if s + AHEAD < TILES:
+                    if LAST_T and cell[0] == TILES - 1:
+                        times_x(*cell)
+                        add_tokens(cell[1], product_of[cell], True)
+                        to_reduce_next.append(cell[1])
+                    elif s < LATE_FROM:
                         times_x(*cell)
                         add_tokens(cell[1], product_of[cell], False)
                         settle(cell[1])
                     else:
                         times_x_late(*cell)
                     counts["finished"] += 1
-                behind = 1 if counts["finished"] < TILES * CHUNKS else 0
-                while counts["summed"] < len(waiting) - behind:
+                if LATE_G or counts["finished"] == TILES * CHUNKS:
+                    due = len(waiting)
+                while counts["summed"] < due:
                     add_late(*waiting[counts["summed"]])
                     counts["summed"] += 1
                 for chunk in to_reduce:
                     reduce_chunk(chunk)
                 to_reduce.clear()
+                to_reduce.extend(to_reduce_next)
+                to_reduce_next.clear()
                 while counts["started"] < len(ready) and counts["started"] - counts["finished"] < 2:
                     multiply(*ready[counts["started"]])
                     counts["started"] += 1
                 for chunk in closing:
-                    add_tokens(chunk, running[:, chunk * N_TILE : (chunk + 1) * N_TILE], True)
-                    to_reduce.append(chunk)
+                    if chunk in running_begun:
+                        add_tokens(chunk, running[:, chunk * N_TILE : (chunk + 1) * N_TILE], not LAST_T)
+                    if not LAST_T:
+                        to_reduce.append(chunk)
                 closing.clear()
                 if s < TILES and i < PASSES:
                     scale_round(s, i)

@@ -36,6 +36,7 @@ HEAD = "new"
 LATE_FROM = 5
 LATE_G = 0
 LAST_T = 1
+DS = 1
 SIGNS_A_STEP = 3
 
 
@@ -309,7 +310,9 @@ def tile_onebitlinear_v_kernel(
                 load_rows(s + AHEAD + 1)
             if s < TILES:
                 load_x(s)
-            for i in range(SLOTS):
+            groups = [[0, 1], [2, 3], [4]] if DS else [[i] for i in range(SLOTS)]
+            for group in groups:
+              for i in group:
                 counts["slot"] += 1
                 if i < SIGNS_A_STEP and counts["unit"] < W_UNITS:
                     weight_signs(counts["unit"])
@@ -321,20 +324,25 @@ def tile_onebitlinear_v_kernel(
                         row_piece(s + AHEAD, i // 2)
                     elif i == 3:
                         straight_line(s + AHEAD)
-                due = len(waiting)
+              due = len(waiting)
+              fresh = []
+              for i in group:
                 if counts["finished"] < counts["started"]:
                     cell = ready[counts["finished"]]
-                    if LAST_T and cell[0] == TILES - 1:
+                    if (LAST_T and cell[0] == TILES - 1) or s < LATE_FROM:
                         times_x(*cell)
-                        add_tokens(cell[1], product_of[cell], True)
-                        to_reduce_next.append(cell[1])
-                    elif s < LATE_FROM:
-                        times_x(*cell)
-                        add_tokens(cell[1], product_of[cell], False)
-                        settle(cell[1])
+                        fresh.append(cell)
                     else:
                         times_x_late(*cell)
                     counts["finished"] += 1
+              for cell in fresh:
+                    if LAST_T and cell[0] == TILES - 1:
+                        add_tokens(cell[1], product_of[cell], True)
+                        to_reduce_next.append(cell[1])
+                    else:
+                        add_tokens(cell[1], product_of[cell], False)
+                        settle(cell[1])
+              if True:
                 if LATE_G or counts["finished"] == TILES * CHUNKS:
                     due = len(waiting)
                 while counts["summed"] < due:
@@ -354,11 +362,15 @@ def tile_onebitlinear_v_kernel(
                     if not LAST_T:
                         to_reduce.append(chunk)
                 closing.clear()
+              for i in group:
                 if s < TILES and i < PASSES:
                     scale_round(s, i)
+              for i in group:
+                if s < TILES and i < PASSES:
                     n_next, c_next = divmod(s * PASSES + i + 2, PASSES)
                     if n_next < TILES:
                         turn(n_next, c_next)
+              for i in group:
                 load = counts["load"]
                 if load < W_LOADS and signed_at.get(load, counts["slot"]) + 2 <= counts["slot"]:
                     quantise_weights(load)

@@ -37,6 +37,10 @@ LATE_FROM = 5
 LATE_G = 0
 LAST_T = 1
 DS = 1
+ADDT_LAST = 1
+SLOTS = 5
+P2_AT = 2
+LINE_AT = 3
 SIGNS_A_STEP = 3
 
 
@@ -310,7 +314,7 @@ def tile_onebitlinear_v_kernel(
                 load_rows(s + AHEAD + 1)
             if s < TILES:
                 load_x(s)
-            groups = [[0, 1], [2, 3], [4]] if DS else [[i] for i in range(SLOTS)]
+            groups = [list(range(a, min(a + 2, SLOTS))) for a in range(0, SLOTS, 2)] if DS else [[i] for i in range(SLOTS)]
             for group in groups:
               for i in group:
                 counts["slot"] += 1
@@ -320,9 +324,11 @@ def tile_onebitlinear_v_kernel(
                         signed_at[counts["unit"] // 2] = counts["slot"]
                     counts["unit"] += 1
                 if s + AHEAD < TILES:
-                    if i in (0, 2):
-                        row_piece(s + AHEAD, i // 2)
-                    elif i == 3:
+                    if i == 0:
+                        row_piece(s + AHEAD, 0)
+                    if i == P2_AT:
+                        row_piece(s + AHEAD, 1)
+                    if i == LINE_AT:
                         straight_line(s + AHEAD)
               due = len(waiting)
               fresh = []
@@ -335,7 +341,7 @@ def tile_onebitlinear_v_kernel(
                     else:
                         times_x_late(*cell)
                     counts["finished"] += 1
-              for cell in fresh:
+              for cell in ([] if ADDT_LAST else fresh):
                     if LAST_T and cell[0] == TILES - 1:
                         add_tokens(cell[1], product_of[cell], True)
                         to_reduce_next.append(cell[1])
@@ -370,6 +376,13 @@ def tile_onebitlinear_v_kernel(
                     n_next, c_next = divmod(s * PASSES + i + 2, PASSES)
                     if n_next < TILES:
                         turn(n_next, c_next)
+              for cell in (fresh if ADDT_LAST else []):
+                    if LAST_T and cell[0] == TILES - 1:
+                        add_tokens(cell[1], product_of[cell], True)
+                        to_reduce_next.append(cell[1])
+                    else:
+                        add_tokens(cell[1], product_of[cell], False)
+                        settle(cell[1])
               for i in group:
                 load = counts["load"]
                 if load < W_LOADS and signed_at.get(load, counts["slot"]) + 2 <= counts["slot"]:

@@ -37,6 +37,10 @@ LATE_FROM = 5
 LATE_G = 0
 LAST_T = 1
 DS = 1
+T_CHUNKS = 2
+TB = 3
+AB = 3
+GS = 2
 ADDT_LAST = 1
 SLOTS = 5
 P2_AT = 2
@@ -53,8 +57,8 @@ def tile_onebitlinear_v_kernel(
         rows = stack.enter_context(tc.tile_pool(name="rows", bufs=3))
         small = stack.enter_context(tc.tile_pool(name="small", bufs=4))
         stage = stack.enter_context(tc.tile_pool(name="stage", bufs=2))
-        turned = stack.enter_context(tc.psum_pool(name="turned", bufs=2))
-        banks = stack.enter_context(tc.psum_pool(name="banks", bufs=2))
+        turned = stack.enter_context(tc.psum_pool(name="turned", bufs=TB))
+        banks = stack.enter_context(tc.psum_pool(name="banks", bufs=AB))
         total = stack.enter_context(tc.psum_pool(name="total", bufs=1))
         stack.enter_context(tc.manual_schedule())
 
@@ -68,7 +72,7 @@ def tile_onebitlinear_v_kernel(
         w_scales = keep.tile([P, CHUNKS, PASSES, N_TILE], U8, align_bytes=64)
         dm_codes = keep.tile([P, TILES, PASSES, P], U32, align_bytes=64)
         dm_scales = keep.tile([P, TILES, PASSES, P], U8, align_bytes=64)
-        token_sums = [total.tile([P, PACK, P], F32, tag="sums%d" % chunk, name="token_sums") for chunk in range(CHUNKS)]
+        token_sums = [total.tile([P, PACK, P], F32, tag="sums%d" % chunk, name="token_sums") for chunk in range(T_CHUNKS)] + [None] * (CHUNKS - T_CHUNKS)
         g_of, h_of, gr_of, sums_of, banks_of, grouped_of = {}, {}, {}, {}, {}, {}
         raw_of, signs_of, acc_of, product_of = {}, {}, {}, {}
         added = [0] * CHUNKS
@@ -302,8 +306,8 @@ def tile_onebitlinear_v_kernel(
             if n == 0 and HEAD != 'old':
                 prepare_ocs()
             if n == 0:
-                turn(0, 0)
-                turn(0, 1)
+                for c in range(TB):
+                    turn(0, c)
 
         ready = []
         counts = {"started": 0, "finished": 0, "unit": 2, "load": 0, "slot": 0, "summed": 0}
@@ -314,7 +318,7 @@ def tile_onebitlinear_v_kernel(
                 load_rows(s + AHEAD + 1)
             if s < TILES:
                 load_x(s)
-            groups = [list(range(a, min(a + 2, SLOTS))) for a in range(0, SLOTS, 2)] if DS else [[i] for i in range(SLOTS)]
+            groups = [list(range(a, min(a + GS, SLOTS))) for a in range(0, SLOTS, GS)] if DS else [[i] for i in range(SLOTS)]
             for group in groups:
               for i in group:
                 counts["slot"] += 1
@@ -335,7 +339,7 @@ def tile_onebitlinear_v_kernel(
               for i in group:
                 if counts["finished"] < counts["started"]:
                     cell = ready[counts["finished"]]
-                    if (LAST_T and cell[0] == TILES - 1) or s < LATE_FROM:
+                    if (LAST_T and cell[0] == TILES - 1) or (s < LATE_FROM if T_CHUNKS == CHUNKS else cell[1] < T_CHUNKS):
                         times_x(*cell)
                         fresh.append(cell)
                     else:
@@ -359,11 +363,11 @@ def tile_onebitlinear_v_kernel(
                 to_reduce.clear()
                 to_reduce.extend(to_reduce_next)
                 to_reduce_next.clear()
-                while counts["started"] < len(ready) and counts["started"] - counts["finished"] < 2:
+                while counts["started"] < len(ready) and counts["started"] - counts["finished"] < AB:
                     multiply(*ready[counts["started"]])
                     counts["started"] += 1
                 for chunk in closing:
-                    if chunk in running_begun:
+                    if chunk in running_begun and T_CHUNKS == CHUNKS:
                         add_tokens(chunk, running[:, chunk * N_TILE : (chunk + 1) * N_TILE], not LAST_T)
                     if not LAST_T:
                         to_reduce.append(chunk)
@@ -373,11 +377,14 @@ def tile_onebitlinear_v_kernel(
                     scale_round(s, i)
               for i in group:
                 if s < TILES and i < PASSES:
-                    n_next, c_next = divmod(s * PASSES + i + 2, PASSES)
+                    n_next, c_next = divmod(s * PASSES + i + TB, PASSES)
                     if n_next < TILES:
                         turn(n_next, c_next)
               for cell in (fresh if ADDT_LAST else []):
                     if LAST_T and cell[0] == TILES - 1:
+                        if cell[1] >= T_CHUNKS:
+                            token_sums[cell[1]] = turned.tile([P, PACK, P], F32, tag="turned", name="token_sums")
+                            add_tokens(cell[1], running[:, cell[1] * N_TILE : (cell[1] + 1) * N_TILE], False)
                         add_tokens(cell[1], product_of[cell], True)
                         to_reduce_next.append(cell[1])
                     else:

@@ -37,6 +37,8 @@ LATE_FROM = 5
 LATE_G = 0
 LAST_T = 1
 DS = 1
+GB = 1
+Q_AT = 4
 T_CHUNKS = 2
 TB = 3
 AB = 3
@@ -262,7 +264,14 @@ def tile_onebitlinear_v_kernel(
             ocs_rows = keep.tile([BLOCKS, P], BF16)
             nc.sync.dma_start(out=rstd_sb[:], in_=rstd.rearrange("(p n) o -> p (n o)", n=TILES))
             load_g(0)
-            nc.sync.dma_start(out=gamma_all[:], in_=ln_gamma.partition_broadcast(P))
+            if GB:
+                gamma_row = keep.tile([P, D_OUT], BF16)
+                nc.vector.memset(gamma_row[:], 0.0)
+                all_ones = keep.tile([P, P], BF16)
+                nc.vector.memset(all_ones[:], 1.0)
+                nc.sync.dma_start(out=gamma_row[0:1, :], in_=ln_gamma.rearrange("(o d) -> o d", o=1))
+            else:
+                nc.sync.dma_start(out=gamma_all[:], in_=ln_gamma.partition_broadcast(P))
             nc.sync.dma_start(out=mu_sb[:], in_=mu.rearrange("(p n) o -> p (n o)", n=TILES))
             load_weights(0, nc.sync)
             load_h(0)
@@ -279,6 +288,15 @@ def tile_onebitlinear_v_kernel(
         nc.vector.memset(ocs_square[:], 0.0)
         out_square = keep.tile([P, P], F32)
         nc.vector.memset(out_square[:], 0.0)
+
+        if GB:
+            for c in range(CHUNKS):
+                spread = banks.tile([P, N_TILE], F32, tag="acc", name="spread")
+                nc.tensor.matmul(out=spread[:], lhsT=all_ones[:], rhs=gamma_row[:, c * N_TILE : (c + 1) * N_TILE], start=True, stop=True)
+                if c % 2 == 0:
+                    nc.vector.tensor_copy(out=gamma_all[:, c * N_TILE : (c + 1) * N_TILE], in_=spread[:])
+                else:
+                    nc.scalar.copy(out=gamma_all[:, c * N_TILE : (c + 1) * N_TILE], in_=spread[:])
 
         slope_of = keep.tile([P, TILES, 2], F32)
         nc.vector.scalar_tensor_tensor(
@@ -398,7 +416,7 @@ def tile_onebitlinear_v_kernel(
                     if load % 2 == 1:
                         chunks_done.append(load // 2)
                         ready.extend([(n, load // 2) for n in tiles_done])
-                if s < TILES and i == SLOTS - 1:
+                if s < TILES and i == Q_AT:
                     quantise_rows(s)
                     tiles_done.append(s)
                     ready.extend([(s, chunk) for chunk in chunks_done])

from contextlib import ExitStack

import concourse.mybir as mybir
from concourse.masks import make_identity

F32 = mybir.dt.float32
BF16 = mybir.dt.bfloat16
U32 = mybir.dt.uint32
U8 = mybir.dt.uint8
E4M3_X4 = mybir.dt.float8_e4m3fn_x4
E5M2_X4 = mybir.dt.float8_e5m2_x4
ALU = mybir.AluOpType
ACT = mybir.ActivationFunctionType
AX = mybir.AxisListType

P = 128
PACK = 4
TOKENS = 1024
D_IN = 2048
D_OUT = 2048
TILES = TOKENS // P
PASSES = D_OUT // (P * PACK)
BLOCKS = D_OUT // P
N_TILE = 512
CHUNKS = D_IN // N_TILE
W_LOADS = 2 * CHUNKS
W_UNITS = 2 * W_LOADS
HALF = D_OUT // 2
SLOTS = 5
SIGNS_A_STEP = 3
AHEAD = 2

FLOPS = 2 * TOKENS * D_IN * D_OUT
TINY = "s"
HEAD = "new"
LATE_FROM = 5
LATE_G = 0
LAST_T = 1
DS = 1
GB = 1
Q_AT = 4
T_CHUNKS = 2
TB = 3
AB = 3
GS = 2
ADDT_LAST = 1
SLOTS = 5
P2_AT = 2
LINE_AT = 3
SIGNS_A_STEP = 3


def tile_onebitlinear_v_kernel(
    tc, x, weight, in_channel_scale, out_channel_scale, bias, ln_gamma, ln_beta, h, mu, rstd, grad_out, out
):
    nc = tc.nc
    with ExitStack() as stack:
        keep = stack.enter_context(tc.tile_pool(name="keep", bufs=1))
        rows = stack.enter_context(tc.tile_pool(name="rows", bufs=3))
        small = stack.enter_context(tc.tile_pool(name="small", bufs=4))
        stage = stack.enter_context(tc.tile_pool(name="stage", bufs=2))
        turned = stack.enter_context(tc.psum_pool(name="turned", bufs=TB))
        banks = stack.enter_context(tc.psum_pool(name="banks", bufs=AB))
        total = stack.enter_context(tc.psum_pool(name="total", bufs=1))
        stack.enter_context(tc.manual_schedule())

        g_view = grad_out.flatten_outer_dims().rearrange("(p n) d -> p n d", n=TILES)
        x_view = x.flatten_outer_dims().rearrange("(p n) d -> p n d", n=TILES)
        h_view = h.rearrange("(p n) d -> p n d", n=TILES)
        w_view = weight.rearrange("(r p) i -> p r i", p=P)

        x_all = keep.tile([P, TILES, D_IN], BF16)
        w_codes = keep.tile([P, CHUNKS, PASSES, N_TILE], U32, align_bytes=64)
        w_scales = keep.tile([P, CHUNKS, PASSES, N_TILE], U8, align_bytes=64)
        dm_codes = keep.tile([P, TILES, PASSES, P], U32, align_bytes=64)
        dm_scales = keep.tile([P, TILES, PASSES, P], U8, align_bytes=64)
        token_sums = [total.tile([P, PACK, P], F32, tag="sums%d" % chunk, name="token_sums") for chunk in range(T_CHUNKS)] + [None] * (CHUNKS - T_CHUNKS)
        g_of, h_of, gr_of, sums_of, banks_of, grouped_of = {}, {}, {}, {}, {}, {}
        raw_of, signs_of, acc_of, product_of = {}, {}, {}, {}
        added = [0] * CHUNKS
        cells_done = [0] * CHUNKS
        running = keep.tile([P, D_IN], F32)
        running_begun, to_reduce, waiting, closing, to_reduce_next = [], [], [], [], []

        def load_g(n):
            g_of[n] = rows.tile([P, D_OUT], BF16, tag="g", name="g_tile")
            nc.sync.dma_start(out=g_of[n][:], in_=g_view[:, n, :])

        def load_h(n):
            h_of[n] = rows.tile([P, D_OUT], F32, tag="h", name="h_tile", bufs=4)
            nc.sync.dma_start(out=h_of[n][:], in_=h_view[:, n, :])

        def load_rows(n):
            load_g(n)
            load_h(n)

        def load_x(n):
            nc.sync.dma_start(out=x_all[:, n, :], in_=x_view[:, n, :])

        def row_piece(n, piece):
            if piece == 0:
                sums_of[n] = small.tile([P, 2], F32, tag="sums", name="sums")
                gr_of[n] = rows.tile([P, D_OUT], F32, tag="gr", name="gr")
                nc.vector.scalar_tensor_tensor(
                    out=gr_of[n][:], in0=g_of[n][:], scalar=rstd_sb[:, n : n + 1], in1=gamma_all[:],
                    op0=ALU.mult, op1=ALU.mult, accum_out=sums_of[n][:, 0:1],
                )
            else:
                unread = stage.tile([P, D_OUT], F32, tag="unread", bufs=1)
                nc.vector.scalar_tensor_tensor(
                    out=unread[:], in0=h_of[n][:], scalar=mu_sb[:, n : n + 1], in1=gr_of[n][:],
                    op0=ALU.subtract, op1=ALU.mult, accum_out=sums_of[n][:, 1:2],
                )

        def straight_line(n):
            both = sums_of[n]
            line = small.tile([P, 3], F32, tag="line")
            te = {'v': nc.vector, 'g': nc.gpsimd}.get(TINY)
            if te:
                te.tensor_scalar(out=line[:, 0:1], in0=both[:, 0:1], scalar1=-1.0 / D_OUT, scalar2=None, op0=ALU.mult)
                te.tensor_scalar(out=line[:, 1:2], in0=both[:, 1:2], scalar1=slope_of[:, n, 0:1], scalar2=None, op0=ALU.mult)
                te.tensor_scalar(
                    out=line[:, 2:3], in0=both[:, 1:2], scalar1=slope_of[:, n, 1:2], scalar2=line[:, 0:1], op0=ALU.mult, op1=ALU.add
                )
            else:
                nc.scalar.activation(out=line[:, 0:1], in_=both[:, 0:1], func=ACT.Copy, scale=-1.0 / D_OUT)
                nc.scalar.activation(out=line[:, 1:2], in_=both[:, 1:2], func=ACT.Copy, scale=slope_of[:, n, 0:1])
                nc.scalar.activation(
                    out=line[:, 2:3], in_=both[:, 1:2], func=ACT.Identity, scale=slope_of[:, n, 1:2], bias=line[:, 0:1]
                )
            nc.scalar.activation(
                out=h_of[n][:], in_=h_of[n][:], func=ACT.Identity, scale=line[:, 1:2], bias=line[:, 2:3]
            )

        def turn(n, c):
            bank = turned.tile([P, PACK, P], F32, tag="turned")
            banks_of[n, c] = bank
            for j in range(PACK):
                cols = slice((c * PACK + j) * P, (c * PACK + j + 1) * P)
                nc.tensor.matmul(
                    out=bank[:, j, :], lhsT=gr_of[n][:, cols], rhs=identity[:], is_transpose=True,
                    start=True, stop=False,
                )
                nc.tensor.matmul(
                    out=bank[:, j, :], lhsT=h_of[n][:, cols], rhs=identity[:], is_transpose=True,
                    start=False, stop=True,
                )

        def scale_round(n, c):
            if c == 0:
                grouped_of[n] = stage.tile([P, PASSES, P, PACK], BF16, tag="grouped", name="grouped", align_bytes=64)
            nc.vector.tensor_tensor(
                out=grouped_of[n][:, c, :, :],
                in0=banks_of[n, c][:].rearrange("p j t -> p t j"),
                in1=ocs_col[:, c * PACK : (c + 1) * PACK].unsqueeze(1).to_broadcast([P, P, PACK]),
                op=ALU.mult,
            )

        def quantise_rows(n):
            nc.vector.quantize_mx(
                out=dm_codes[:, n, :, :].rearrange("p c t -> p (c t)").bitcast(E5M2_X4),
                scales=dm_scales[:, n, :, :].rearrange("p c t -> p (c t)"),
                in_=grouped_of[n][:].rearrange("p c t j -> p (c t j)"),
            )

        def load_weights(load, queue=None):
            chunk, half = divmod(load, 2)
            raw_of[load] = stage.tile([P, 2, PACK, N_TILE], BF16, tag="raw", name="raw")
            (queue or nc.scalar).dma_start(
                out=raw_of[load][:].rearrange("p k j i -> p (k j) i"),
                in_=w_view[:, half * 2 * PACK : (half + 1) * 2 * PACK, chunk * N_TILE : (chunk + 1) * N_TILE],
            )

        def weight_signs(unit):
            load, k = divmod(unit, 2)
            if k == 0:
                signs_of[load] = stage.tile([P, 2, N_TILE, PACK], BF16, tag="signs", name="signs", align_bytes=64)
            nc.scalar.activation(
                out=signs_of[load][:, k, :, :].rearrange("p (u i) j -> p u j i", i=4),
                in_=raw_of[load][:, k, :, :].rearrange("p j (u i) -> p u j i", i=4),
                func=ACT.Sign, scale=2.0**120, bias=2.0**-20,
            )
            if k == 1 and load + 2 < W_LOADS:
                load_weights(load + 2)

        def quantise_weights(load):
            chunk, half = divmod(load, 2)
            passes = slice(2 * half, 2 * half + 2)
            nc.vector.quantize_mx(
                out=w_codes[:, chunk, passes, :].rearrange("p c i -> p (c i)").bitcast(E4M3_X4),
                scales=w_scales[:, chunk, passes, :].rearrange("p c i -> p (c i)"),
                in_=signs_of[load][:].rearrange("p k i j -> p (k i j)"),
            )

        def multiply(n, chunk):
            acc_of[n, chunk] = banks.tile([P, N_TILE], F32, tag="acc", name="acc")
            for c in range(PASSES):
                nc.tensor.matmul_mx(
                    out=acc_of[n, chunk][:],
                    lhsT=dm_codes[:, n, c, :].bitcast(E5M2_X4),
                    lhsT_scale=dm_scales[:, n, c, :],
                    rhs=w_codes[:, chunk, c, :].bitcast(E4M3_X4),
                    rhs_scale=w_scales[:, chunk, c, :],
                    start=(c == 0),
                    stop=(c == PASSES - 1),
                )

        def times_x(n, chunk):
            cols = slice(chunk * N_TILE, (chunk + 1) * N_TILE)
            product_of[n, chunk] = stage.tile([P, N_TILE], F32, tag="product", name="product", bufs=4)
            nc.vector.tensor_tensor(out=product_of[n, chunk][:], in0=acc_of[n, chunk][:], in1=x_all[:, n, cols], op=ALU.mult)

        def add_tokens(chunk, product, last):
            for b in range(PACK):
                added[chunk] += 1
                nc.tensor.matmul(
                    out=token_sums[chunk][:, b, :], lhsT=product[:, b * P : (b + 1) * P], rhs=identity[:],
                    is_transpose=True, start=(added[chunk] == 1), stop=(last and b == PACK - 1),
                )

        def times_x_late(n, chunk):
            cols = slice(chunk * N_TILE, (chunk + 1) * N_TILE)
            if chunk not in running_begun:
                running_begun.append(chunk)
                nc.vector.tensor_tensor(out=running[:, cols], in0=acc_of[n, chunk][:], in1=x_all[:, n, cols], op=ALU.mult)
                settle(chunk)
            else:
                times_x(n, chunk)
                waiting.append((n, chunk))

        def add_late(n, chunk):
            cols = slice(chunk * N_TILE, (chunk + 1) * N_TILE)
            (nc.gpsimd if LATE_G else nc.vector).tensor_tensor(out=running[:, cols], in0=running[:, cols], in1=product_of[n, chunk][:], op=ALU.add)
            settle(chunk)

        def settle(chunk):
            cells_done[chunk] += 1
            if cells_done[chunk] == TILES - LAST_T:
                closing.append(chunk)

        def reduce_chunk(chunk):
            nc.vector.tensor_reduce(
                out=out_square[:, chunk * PACK : (chunk + 1) * PACK], in_=token_sums[chunk][:], op=ALU.add, axis=AX.X
            )

        if HEAD == 'old':
            rstd_sb = keep.tile([P, TILES], F32)
            nc.sync.dma_start(out=rstd_sb[:], in_=rstd.rearrange("(p n) o -> p (n o)", n=TILES))
            mu_sb = keep.tile([P, TILES], F32)
            nc.sync.dma_start(out=mu_sb[:], in_=mu.rearrange("(p n) o -> p (n o)", n=TILES))
            gamma_all = keep.tile([P, D_OUT], BF16)
            nc.scalar.dma_start(out=gamma_all[:], in_=ln_gamma.partition_broadcast(P))
            ocs_rows = keep.tile([BLOCKS, P], BF16)
            nc.sync.dma_start(out=ocs_rows[:], in_=out_channel_scale.rearrange("(b p) -> b p", p=P))
            load_rows(0)
            load_weights(0)
            load_rows(1)
            load_weights(1)
            load_rows(2)
        else:
            rstd_sb = keep.tile([P, TILES], F32)
            mu_sb = keep.tile([P, TILES], F32)
            gamma_all = keep.tile([P, D_OUT], BF16)
            ocs_rows = keep.tile([BLOCKS, P], BF16)
            nc.sync.dma_start(out=rstd_sb[:], in_=rstd.rearrange("(p n) o -> p (n o)", n=TILES))
            load_g(0)
            if GB:
                gamma_row = keep.tile([P, D_OUT], BF16)
                nc.vector.memset(gamma_row[:], 0.0)
                all_ones = keep.tile([P, P], BF16)
                nc.vector.memset(all_ones[:], 1.0)
                nc.sync.dma_start(out=gamma_row[0:1, :], in_=ln_gamma.rearrange("(o d) -> o d", o=1))
            else:
                nc.sync.dma_start(out=gamma_all[:], in_=ln_gamma.partition_broadcast(P))
            nc.sync.dma_start(out=mu_sb[:], in_=mu.rearrange("(p n) o -> p (n o)", n=TILES))
            load_weights(0, nc.sync)
            load_h(0)
            nc.sync.dma_start(out=ocs_rows[:], in_=out_channel_scale.rearrange("(b p) -> b p", p=P))
            load_g(1)
            load_h(1)
            load_weights(1, nc.sync)
            load_g(2)
            load_h(2)

        identity = keep.tile([P, P], F32)
        make_identity(nc, identity[:])
        ocs_square = keep.tile([P, P], F32)
        nc.vector.memset(ocs_square[:], 0.0)
        out_square = keep.tile([P, P], F32)
        nc.vector.memset(out_square[:], 0.0)

        if GB:
            for c in range(CHUNKS):
                spread = banks.tile([P, N_TILE], F32, tag="acc", name="spread")
                nc.tensor.matmul(out=spread[:], lhsT=all_ones[:], rhs=gamma_row[:, c * N_TILE : (c + 1) * N_TILE], start=True, stop=True)
                if c % 2 == 0:
                    nc.vector.tensor_copy(out=gamma_all[:, c * N_TILE : (c + 1) * N_TILE], in_=spread[:])
                else:
                    nc.scalar.copy(out=gamma_all[:, c * N_TILE : (c + 1) * N_TILE], in_=spread[:])

        slope_of = keep.tile([P, TILES, 2], F32)
        nc.vector.scalar_tensor_tensor(
            out=slope_of[:, :, 0], in0=rstd_sb[:], scalar=-1.0 / D_OUT, in1=rstd_sb[:], op0=ALU.mult, op1=ALU.mult
        )
        nc.vector.scalar_tensor_tensor(
            out=slope_of[:, :, 1], in0=slope_of[:, :, 0], scalar=-1.0, in1=mu_sb[:], op0=ALU.mult, op1=ALU.mult
        )

        def prepare_ocs():
            nc.vector.tensor_copy(out=ocs_square[0:BLOCKS, :], in_=ocs_rows[:])
            ocs_turned = turned.tile([P, PACK, P], F32, tag="turned")
            nc.tensor.transpose(ocs_turned[:, 0, :], ocs_square[:], identity[:])
            nc.vector.tensor_copy(out=ocs_col[:], in_=ocs_turned[:, 0, 0:BLOCKS])

        ocs_col = keep.tile([P, BLOCKS], F32)
        if HEAD == 'old':
            prepare_ocs()
        weight_signs(0)
        weight_signs(1)
        for n in range(AHEAD):
            for piece in range(2):
                row_piece(n, piece)
            straight_line(n)
            if n == 0 and HEAD != 'old':
                prepare_ocs()
            if n == 0:
                for c in range(TB):
                    turn(0, c)

        ready = []
        counts = {"started": 0, "finished": 0, "unit": 2, "load": 0, "slot": 0, "summed": 0}
        signed_at = {0: 0}
        tiles_done, chunks_done = [], []
        for s in range(TILES + 3):
            if s + AHEAD + 1 < TILES:
                load_rows(s + AHEAD + 1)
            if s < TILES:
                load_x(s)
            groups = [list(range(a, min(a + GS, SLOTS))) for a in range(0, SLOTS, GS)] if DS else [[i] for i in range(SLOTS)]
            for group in groups:
              for i in group:
                counts["slot"] += 1
                if i < SIGNS_A_STEP and counts["unit"] < W_UNITS:
                    weight_signs(counts["unit"])
                    if counts["unit"] % 2 == 1:
                        signed_at[counts["unit"] // 2] = counts["slot"]
                    counts["unit"] += 1
                if s + AHEAD < TILES:
                    if i == 0:
                        row_piece(s + AHEAD, 0)
                    if i == P2_AT:
                        row_piece(s + AHEAD, 1)
                    if i == LINE_AT:
                        straight_line(s + AHEAD)
              due = len(waiting)
              fresh = []
              for i in group:
                if counts["finished"] < counts["started"]:
                    cell = ready[counts["finished"]]
                    if (LAST_T and cell[0] == TILES - 1) or (s < LATE_FROM if T_CHUNKS == CHUNKS else cell[1] < T_CHUNKS):
                        times_x(*cell)
                        fresh.append(cell)
                    else:
                        times_x_late(*cell)
                    counts["finished"] += 1
              for cell in ([] if ADDT_LAST else fresh):
                    if LAST_T and cell[0] == TILES - 1:
                        add_tokens(cell[1], product_of[cell], True)
                        to_reduce_next.append(cell[1])
                    else:
                        add_tokens(cell[1], product_of[cell], False)
                        settle(cell[1])
              if True:
                if LATE_G or counts["finished"] == TILES * CHUNKS:
                    due = len(waiting)
                while counts["summed"] < due:
                    add_late(*waiting[counts["summed"]])
                    counts["summed"] += 1
                for chunk in to_reduce:
                    reduce_chunk(chunk)
                to_reduce.clear()
                to_reduce.extend(to_reduce_next)
                to_reduce_next.clear()
                while counts["started"] < len(ready) and counts["started"] - counts["finished"] < AB:
                    multiply(*ready[counts["started"]])
                    counts["started"] += 1
                for chunk in closing:
                    if chunk in running_begun and T_CHUNKS == CHUNKS:
                        add_tokens(chunk, running[:, chunk * N_TILE : (chunk + 1) * N_TILE], not LAST_T)
                    if not LAST_T:
                        to_reduce.append(chunk)
                closing.clear()
              for i in group:
                if s < TILES and i < PASSES:
                    scale_round(s, i)
              for i in group:
                if s < TILES and i < PASSES:
                    n_next, c_next = divmod(s * PASSES + i + TB, PASSES)
                    if n_next < TILES:
                        turn(n_next, c_next)
              for cell in (fresh if ADDT_LAST else []):
                    if LAST_T and cell[0] == TILES - 1:
                        if cell[1] >= T_CHUNKS:
                            token_sums[cell[1]] = turned.tile([P, PACK, P], F32, tag="turned", name="token_sums")
                            add_tokens(cell[1], running[:, cell[1] * N_TILE : (cell[1] + 1) * N_TILE], False)
                        add_tokens(cell[1], product_of[cell], True)
                        to_reduce_next.append(cell[1])
                    else:
                        add_tokens(cell[1], product_of[cell], False)
                        settle(cell[1])
              for i in group:
                load = counts["load"]
                if load < W_LOADS and signed_at.get(load, counts["slot"]) + 2 <= counts["slot"]:
                    quantise_weights(load)
                    counts["load"] += 1
                    if load % 2 == 1:
                        chunks_done.append(load // 2)
                        ready.extend([(n, load // 2) for n in tiles_done])
                if s < TILES and i == Q_AT:
                    quantise_rows(s)
                    tiles_done.append(s)
                    ready.extend([(s, chunk) for chunk in chunks_done])
        assert counts["finished"] == TILES * CHUNKS

        assert not to_reduce
        out_turned = turned.tile([P, PACK, P], F32, tag="turned")
        nc.tensor.transpose(out_turned[:, 0, :], out_square[:], identity[:])
        result = keep.tile([P, P], F32)
        nc.vector.tensor_copy(out=result[:], in_=out_turned[:, 0, :])
        nc.sync.dma_start(out=out.rearrange("(c p) -> c p", p=P), in_=result[0 : CHUNKS * PACK, :])
